import numpy as np
import ml_dtypes


def mxq(x, axis, fmt="e4m3"):
    dtype, down = {"e4m3": (ml_dtypes.float8_e4m3fn, 7), "e5m2": (ml_dtypes.float8_e5m2, 14)}[fmt]
    v = np.moveaxis(np.asarray(x, np.float32).astype(ml_dtypes.bfloat16).astype(np.float64), axis, -1)
    blocks = v.reshape(v.shape[:-1] + (-1, 32))
    amax = np.abs(blocks).max(-1, keepdims=True)
    byte = np.maximum(np.where(amax > 0, np.frexp(amax)[1] - 1 + 127, 0) - down, 1)
    scale = np.exp2(byte - 127.0)
    codes = (blocks / scale).astype(np.float32).astype(dtype).astype(np.float64)
    return np.moveaxis((codes * scale).reshape(v.shape), -1, axis)


BF16 = ml_dtypes.bfloat16


def bf(x):
    return np.asarray(x, np.float32).astype(BF16)


def f64(x):
    return np.asarray(x).astype(np.float64)


B, C, H, W = 4, 512, 32, 32
N = H * W
NEG_INF = -1.0e9
SIG = np.sqrt(np.log(0.6 * N) / np.sqrt(C))
GRID = 0.0625


def setup_inputs():
    return {"x": bf(np.round(np.random.standard_normal((B, C, H, W)) * SIG / GRID) * GRID), "threshold": 0.05}


def reference(x, threshold):
    feat = f64(x).reshape(B, C, N)
    scale = np.sqrt(C)
    affinity = feat.transpose(0, 2, 1) @ feat / scale
    affinity = np.where(affinity < threshold, NEG_INF, affinity)
    e = np.exp(affinity - affinity.max(-1, keepdims=True))
    out = (mxq(e, 2, "e4m3") @ mxq(feat, 2, "e4m3").transpose(0, 2, 1)) / e.sum(-1, keepdims=True)
    return out.transpose(0, 2, 1).reshape(B, C, H, W)

@@ -1,0 +1,254 @@
+import math
+from contextlib import ExitStack
+
+import concourse.mybir as mybir
+from concourse.masks import make_identity
+
+F32 = mybir.dt.float32
+BF16 = mybir.dt.bfloat16
+U32 = mybir.dt.uint32
+U8 = mybir.dt.uint8
+FP8X4 = mybir.dt.float8_e4m3fn_x4
+ALU = mybir.AluOpType
+ACT = mybir.ActivationFunctionType
+
+P = 128
+B = 4
+C = 512
+N = 1024
+NCC = C // P
+NRB = N // P
+HALF = 512
+FLOPS = 2 * 2 * B * N * N * C
+
+
+def threshold_pair(t):
+    unit = 1.0
+    while t / unit >= 16777216.0:
+        unit = unit * 2.0
+    while t / unit < 8388608.0:
+        unit = unit / 2.0
+    y = t / unit
+    lo = int(y)
+    if lo == y:
+        lo = lo - 1
+    return lo * unit, (lo + 1) * unit
+
+
+def tile_sapmodule_t_kernel(tc, x, threshold, out):
+    nc = tc.nc
+    assert threshold > 0.0
+    scale = 1.0 / math.sqrt(C)
+    t_lo, t_hi = threshold_pair(threshold * math.sqrt(C))
+
+    xv = x.rearrange("b (p cc) h w -> b p cc (h w)", cc=NCC)
+    ov = out.rearrange("b (m cc) h w -> b m cc (h w)", cc=NCC)
+
+    with ExitStack() as ctx:
+        const = ctx.enter_context(tc.tile_pool(name="const", bufs=1))
+        xpool = ctx.enter_context(tc.tile_pool(name="xpool", bufs=1))
+        work = ctx.enter_context(tc.tile_pool(name="work", bufs=3))
+        small = ctx.enter_context(tc.tile_pool(name="small", bufs=4))
+        mxp = ctx.enter_context(tc.tile_pool(name="mxp", bufs=2))
+        ps_s = ctx.enter_context(tc.psum_pool(name="ps_s", bufs=4))
+        ps_t = ctx.enter_context(tc.psum_pool(name="ps_t", bufs=2))
+        ps_o = ctx.enter_context(tc.psum_pool(name="ps_o", bufs=2))
+
+        xs = []
+        for b in range(B):
+            xt = xpool.tile([P, NCC, N], BF16, name="x%d" % b)
+            xs.append(xt)
+            if b == 0:
+                for cc in range(NCC):
+                    nc.sync.dma_start(out=xt[:, cc, :], in_=xv[b][:, cc, :])
+            else:
+                nc.sync.dma_start(out=xt[:], in_=xv[b])
+
+        ident_bf = const.tile([P, P], BF16, name="ident_bf")
+        make_identity(nc, ident_bf[:])
+        ident_f = const.tile([P, P], F32, name="ident_f")
+        make_identity(nc, ident_f[:])
+
+        st = {}
+
+        def s_bank(s, g):
+            b, r = divmod(s, NRB)
+            xp = xs[b][:].rearrange("p cc (r q e) -> p cc r e q", q=P, e=2)
+            sps = ps_s.tile([P, HALF], F32, name="sps", tag="sps")
+            st[("sps", s, g)] = sps
+            for cc in range(NCC):
+                nc.tensor.matmul(
+                    out=sps[:].rearrange("p (u e q) -> p u e q", u=2, e=2),
+                    lhsT=xp[:, cc, r // 2, r % 2, :],
+                    rhs=xp[:, cc, 2 * g : 2 * g + 2, :, :],
+                    start=(cc == 0),
+                    stop=(cc == NCC - 1),
+                )
+
+        def clamp_max(s, g):
+            if g == 0:
+                st[("c", s)] = work.tile([P, N], F32, name="cl", tag="cl")
+                st[("mx", s)] = small.tile([P, 2], F32, name="mx", tag="mx")
+            nc.vector.tensor_scalar(
+                out=st[("c", s)][:, g * HALF : (g + 1) * HALF],
+                in0=st[("sps", s, g)][:],
+                scalar1=t_lo,
+                scalar2=None,
+                op0=ALU.max,
+                op1=ALU.max,
+                accum_out=st[("mx", s)][:, g : g + 1],
+            )
+
+        def row_scalars(s):
+            mx = st[("mx", s)]
+            negm = small.tile([P, 1], F32, name="negm", tag="negm")
+            nc.vector.tensor_scalar(
+                out=negm[:], in0=mx[:, 0:1], scalar1=mx[:, 1:2], scalar2=-scale,
+                op0=ALU.max, op1=ALU.mult,
+            )
+            thr = small.tile([P, 1], F32, name="thr", tag="thr")
+            nc.gpsimd.tensor_scalar(
+                out=thr[:], in0=mx[:, 0:1], scalar1=mx[:, 1:2], scalar2=t_hi,
+                op0=ALU.max, op1=ALU.min,
+            )
+            st[("negm", s)] = negm
+            st[("thr", s)] = thr
+
+        def exp_row(s):
+            e2 = work.tile([P, N], F32, name="e2", tag="e2")
+            nc.scalar.activation(
+                out=e2[:], in_=st[("c", s)][:], func=ACT.Exp,
+                bias=st[("negm", s)][:, 0:1], scale=scale,
+            )
+            st[("e2", s)] = e2
+
+        def mask_sum(s):
+            h, rl = divmod(s, 4)
+            if rl == 0:
+                st[("ssum", h)] = small.tile([P, 4], F32, name="ssum", tag="ssum")
+            ebf = work.tile([P, N], BF16, name="ebf", tag="ebf")
+            nc.vector.scalar_tensor_tensor(
+                out=ebf[:], in0=st[("c", s)][:], scalar=st[("thr", s)][:, 0:1],
+                in1=st[("e2", s)][:], op0=ALU.is_ge, op1=ALU.mult,
+                accum_out=st[("ssum", h)][:, rl : rl + 1],
+            )
+            st[("ebf", s)] = ebf
+
+        def e_transposes(s):
+            tp = ps_t.tile([P, NRB, P], BF16, name="tp", tag="tp")
+            ebf = st[("ebf", s)]
+            for k in range(NRB):
+                nc.tensor.transpose(tp[:, k, :], ebf[:, k * P : (k + 1) * P], ident_bf[:])
+            st[("tp", s)] = tp
+
+        def e_regroup(s):
+            h, rl = divmod(s, 4)
+            if rl == 0:
+                st[("grp", h)] = mxp.tile([P, 2, HALF, 4], BF16, name="grp", tag="grp", align_bytes=64)
+            nc.scalar.copy(
+                out=st[("grp", h)][:, :, rl * P : (rl + 1) * P, :],
+                in_=st[("tp", s)][:].rearrange("p (g t) i -> p g i t", g=2),
+            )
+
+        def e_quant(h):
+            ecod = mxp.tile([P, 2 * HALF], U32, name="ecod", tag="ecod", align_bytes=64)
+            esc = mxp.tile([P, 2 * HALF], U8, name="esc", tag="esc", align_bytes=64)
+            nc.vector.quantize_mx(
+                out=ecod[:].bitcast(FP8X4), scales=esc[:],
+                in_=st[("grp", h)][:].rearrange("p g n t -> p (g n t)"),
+            )
+            st[("ecod", h)] = ecod
+            st[("esc", h)] = esc
+
+        def f_transposes(b, g, cp):
+            xw = xs[b][:].rearrange("p cc n -> p (cc n)").bitcast(F32)
+            ft = ps_t.tile([P, 2, 2 * P], F32, name="ft", tag="tp")
+            for u in range(2):
+                for c2 in range(2):
+                    cc = 2 * cp + c2
+                    w0 = cc * (N // 2) + (2 * g + u) * P
+                    nc.tensor.transpose(ft[:, u, c2 * P : (c2 + 1) * P], xw[:, w0 : w0 + P], ident_f[:])
+            if g == 0 and cp == 0:
+                st[("fgrp", b)] = mxp.tile([P, 4 * N], BF16, name="fgrp", tag="fgrp", align_bytes=64)
+            fgw = st[("fgrp", b)][:].bitcast(F32).rearrange("p (g c u) -> p g c u", g=2, u=2)
+            nc.scalar.copy(
+                out=fgw[:, g, cp * 2 * P : (cp + 1) * 2 * P, :],
+                in_=ft[:].rearrange("p u c -> p c u"),
+            )
+
+        def f_quant(b):
+            fcod = mxp.tile([P, 2 * C], U32, name="fcod", tag="fcod", align_bytes=64)
+            fsc = mxp.tile([P, 2 * C], U8, name="fsc", tag="fsc", align_bytes=64)
+            nc.vector.quantize_mx(out=fcod[:].bitcast(FP8X4), scales=fsc[:], in_=st[("fgrp", b)][:])
+            st[("fcod", b)] = fcod
+            st[("fsc", b)] = fsc
+
+        def rs_broadcast(h):
+            rsv = small.tile([P, 4], F32, name="rsv", tag="rsv")
+            nc.vector.reciprocal(out=rsv[:], in_=st[("ssum", h)][:])
+            bc = ps_t.tile([P, HALF], F32, name="bc", tag="tp")
+            for rl in range(4):
+                nc.tensor.transpose(
+                    bc[:, rl * P : (rl + 1) * P], rsv[:, rl : rl + 1].to_broadcast([P, P]), ident_f[:]
+                )
+            rsb = mxp.tile([P, HALF], F32, name="rsb", tag="rsb")
+            nc.scalar.copy(out=rsb[:], in_=bc[:])
+            st[("rsb", h)] = rsb
+
+        def mx_block(h, cc):
+            b = h // 2
+            acc = ps_o.tile([P, HALF], F32, name="acc", tag="acc")
+            for g in range(2):
+                nc.tensor.matmul_mx(
+                    out=acc[:],
+                    lhsT=st[("fcod", b)][:, g * C + cc * P : g * C + (cc + 1) * P].bitcast(FP8X4),
+                    lhsT_scale=st[("fsc", b)][:, g * C + cc * P : g * C + (cc + 1) * P],
+                    rhs=st[("ecod", h)][:, g * HALF : (g + 1) * HALF].bitcast(FP8X4),
+                    rhs_scale=st[("esc", h)][:, g * HALF : (g + 1) * HALF],
+                    start=(g == 0),
+                    stop=(g == 1),
+                )
+            st[("acc", h, cc)] = acc
+
+        def normalise(h, cc):
+            if cc == 0:
+                st[("osb", h)] = work.tile([P, NCC, HALF], F32, name="osb", tag="osb")
+            nc.vector.tensor_tensor(
+                out=st[("osb", h)][:, cc, :].rearrange("p (u q e) -> p u q e", u=2, e=2),
+                in0=st[("acc", h, cc)][:].rearrange("p (u e q) -> p u q e", u=2, e=2),
+                in1=st[("rsb", h)][:].rearrange("p (u e q) -> p u q e", u=2, e=2),
+                op=ALU.mult,
+            )
+            if cc == NCC - 1:
+                b, hh = divmod(h, 2)
+                nc.sync.dma_start(out=ov[b][:, :, hh * HALF : (hh + 1) * HALF], in_=st[("osb", h)][:])
+
+        NS = B * NRB
+        for t in range(NS + 11):
+            if t % NRB in (1, 2, 3, 4) and t // NRB < B:
+                k = t % NRB - 1
+                f_transposes(t // NRB, k // 2, k % 2)
+            if t % NRB == 5 and t // NRB < B:
+                f_quant(t // NRB)
+            if t >= 6 and (t - 6) % 4 == 0 and (t - 6) // 4 < 2 * B:
+                rs_broadcast((t - 6) // 4)
+            if 0 <= t - 2 < NS:
+                e_transposes(t - 2)
+                e_regroup(t - 2)
+            if t >= 6 and (t - 6) % 4 == 0 and (t - 6) // 4 < 2 * B:
+                e_quant((t - 6) // 4)
+            if t < NS:
+                s_bank(t, 0)
+            if t >= 7 and (t - 7) // 4 < 2 * B:
+                mx_block((t - 7) // 4, (t - 7) % 4)
+            if t < NS:
+                s_bank(t, 1)
+                clamp_max(t, 0)
+            if 0 <= t - 1 < NS:
+                mask_sum(t - 1)
+            if t < NS:
+                clamp_max(t, 1)
+                row_scalars(t)
+                exp_row(t)
+            if t >= 7 and (t - 7) // 4 < 2 * B:
+                normalise((t - 7) // 4, (t - 7) % 4)

@@ -48,6 +48,7 @@ def tile_sapmodule_t_kernel(tc, x, threshold, out):
         const = ctx.enter_context(tc.tile_pool(name="const", bufs=1))
         xpool = ctx.enter_context(tc.tile_pool(name="xpool", bufs=1))
         work = ctx.enter_context(tc.tile_pool(name="work", bufs=3))
+        clp = ctx.enter_context(tc.tile_pool(name="clp", bufs=11))
         small = ctx.enter_context(tc.tile_pool(name="small", bufs=4))
         mxp = ctx.enter_context(tc.tile_pool(name="mxp", bufs=2))
         ps_s = ctx.enter_context(tc.psum_pool(name="ps_s", bufs=4))
@@ -71,29 +72,51 @@ def tile_sapmodule_t_kernel(tc, x, threshold, out):
 
         st = {}
 
-        def s_bank(s, g):
+        def s_matmuls(s, g):
             b, r = divmod(s, NRB)
             xp = xs[b][:].rearrange("p cc (r q e) -> p cc r e q", q=P, e=2)
             sps = ps_s.tile([P, HALF], F32, name="sps", tag="sps")
             st[("sps", s, g)] = sps
-            for cc in range(NCC):
-                nc.tensor.matmul(
-                    out=sps[:].rearrange("p (u e q) -> p u e q", u=2, e=2),
-                    lhsT=xp[:, cc, r // 2, r % 2, :],
-                    rhs=xp[:, cc, 2 * g : 2 * g + 2, :, :],
-                    start=(cc == 0),
-                    stop=(cc == NCC - 1),
+            k_first = max(r - 4 * g, 0)
+            groups = {0: [(0, 4)], 1: [(1, 2), (2, 4)], 2: [(2, 4)], 3: [(3, 4)]}.get(k_first, [])
+            for k0, k1 in groups:
+                for cc in range(NCC):
+                    if k1 - k0 == 4:
+                        rhs = xp[:, cc, 2 * g : 2 * g + 2, :, :]
+                        dst = sps[:].rearrange("p (u e q) -> p u e q", u=2, e=2)
+                    elif k1 - k0 == 2:
+                        rhs = xp[:, cc, 2 * g + 1, :, :]
+                        dst = sps[:, k0 * P : k1 * P].rearrange("p (e q) -> p e q", e=2)
+                    else:
+                        rhs = xp[:, cc, 2 * g + k0 // 2, 1, :]
+                        dst = sps[:, k0 * P : k1 * P]
+                    nc.tensor.matmul(
+                        out=dst,
+                        lhsT=xp[:, cc, r // 2, r % 2, :],
+                        rhs=rhs,
+                        start=(cc == 0),
+                        stop=(cc == NCC - 1),
+                    )
+
+        def s_mirror(s, g):
+            b, r = divmod(s, NRB)
+            sps = st[("sps", s, g)]
+            for k in range(min(max(r - 4 * g, 0), 4)):
+                nc.tensor.transpose(
+                    sps[:, k * P : (k + 1) * P],
+                    st[("c", b * NRB + 4 * g + k)][:, r * P : (r + 1) * P],
+                    ident_f[:],
                 )
 
         def clamp_max(s, g):
             if g == 0:
-                st[("c", s)] = work.tile([P, N], F32, name="cl", tag="cl")
+                st[("c", s)] = clp.tile([P, N], F32, name="cl", tag="cl")
                 st[("mx", s)] = small.tile([P, 2], F32, name="mx", tag="mx")
             nc.vector.tensor_scalar(
                 out=st[("c", s)][:, g * HALF : (g + 1) * HALF],
                 in0=st[("sps", s, g)][:],
                 scalar1=t_lo,
-                scalar2=None,
+                scalar2=(None if g == 0 else st[("mx", s)][:, 0:1]),
                 op0=ALU.max,
                 op1=ALU.max,
                 accum_out=st[("mx", s)][:, g : g + 1],
@@ -102,14 +125,10 @@ def tile_sapmodule_t_kernel(tc, x, threshold, out):
         def row_scalars(s):
             mx = st[("mx", s)]
             negm = small.tile([P, 1], F32, name="negm", tag="negm")
-            nc.vector.tensor_scalar(
-                out=negm[:], in0=mx[:, 0:1], scalar1=mx[:, 1:2], scalar2=-scale,
-                op0=ALU.max, op1=ALU.mult,
-            )
+            nc.scalar.mul(out=negm[:], in_=mx[:, 1:2], mul=-scale)
             thr = small.tile([P, 1], F32, name="thr", tag="thr")
             nc.gpsimd.tensor_scalar(
-                out=thr[:], in0=mx[:, 0:1], scalar1=mx[:, 1:2], scalar2=t_hi,
-                op0=ALU.max, op1=ALU.min,
+                out=thr[:], in0=mx[:, 1:2], scalar1=t_hi, scalar2=None, op0=ALU.min,
             )
             st[("negm", s)] = negm
             st[("thr", s)] = thr
@@ -238,11 +257,13 @@ def tile_sapmodule_t_kernel(tc, x, threshold, out):
             if t >= 6 and (t - 6) % 4 == 0 and (t - 6) // 4 < 2 * B:
                 e_quant((t - 6) // 4)
             if t < NS:
-                s_bank(t, 0)
+                s_matmuls(t, 0)
             if t >= 7 and (t - 7) // 4 < 2 * B:
                 mx_block((t - 7) // 4, (t - 7) % 4)
             if t < NS:
-                s_bank(t, 1)
+                s_matmuls(t, 1)
+                s_mirror(t, 0)
+                s_mirror(t, 1)
                 clamp_max(t, 0)
             if 0 <= t - 1 < NS:
                 mask_sum(t - 1)

@@ -202,9 +202,13 @@ def tile_sapmodule_t_kernel(tc, x, threshold, out):
             st[("fcod", b)] = fcod
             st[("fsc", b)] = fsc
 
-        def rs_broadcast(h):
+        def rs_recip(h):
             rsv = small.tile([P, 4], F32, name="rsv", tag="rsv")
             nc.vector.reciprocal(out=rsv[:], in_=st[("ssum", h)][:])
+            st[("rsv", h)] = rsv
+
+        def rs_broadcast(h):
+            rsv = st[("rsv", h)]
             bc = ps_t.tile([P, HALF], F32, name="bc", tag="tp")
             for rl in range(4):
                 nc.tensor.transpose(
@@ -238,38 +242,45 @@ def tile_sapmodule_t_kernel(tc, x, threshold, out):
                 in1=st[("rsb", h)][:].rearrange("p (u e q) -> p u q e", u=2, e=2),
                 op=ALU.mult,
             )
-            if cc == NCC - 1:
-                b, hh = divmod(h, 2)
+            b, hh = divmod(h, 2)
+            if h == 2 * B - 1:
+                nc.sync.dma_start(out=ov[b][:, cc, hh * HALF : (hh + 1) * HALF], in_=st[("osb", h)][:, cc, :])
+            elif cc == NCC - 1:
                 nc.sync.dma_start(out=ov[b][:, :, hh * HALF : (hh + 1) * HALF], in_=st[("osb", h)][:])
 
         NS = B * NRB
-        for t in range(NS + 11):
-            if t % NRB in (1, 2, 3, 4) and t // NRB < B:
-                k = t % NRB - 1
-                f_transposes(t // NRB, k // 2, k % 2)
-            if t % NRB == 5 and t // NRB < B:
-                f_quant(t // NRB)
-            if t >= 6 and (t - 6) % 4 == 0 and (t - 6) // 4 < 2 * B:
-                rs_broadcast((t - 6) // 4)
+        NH = 2 * B
+        ctx.enter_context(tc.manual_schedule())
+        for t in range(-1, NS + 9):
+            if 0 <= t < NS:
+                s_mirror(t, 0)
+                s_mirror(t, 1)
             if 0 <= t - 2 < NS:
                 e_transposes(t - 2)
                 e_regroup(t - 2)
-            if t >= 6 and (t - 6) % 4 == 0 and (t - 6) // 4 < 2 * B:
-                e_quant((t - 6) // 4)
-            if t < NS:
-                s_matmuls(t, 0)
-            if t >= 7 and (t - 7) // 4 < 2 * B:
-                mx_block((t - 7) // 4, (t - 7) % 4)
-            if t < NS:
-                s_matmuls(t, 1)
-                s_mirror(t, 0)
-                s_mirror(t, 1)
+            if 0 <= t < NS and t % NRB in (0, 2, 3, 4):
+                k = (0, 2, 3, 4).index(t % NRB)
+                f_transposes(t // NRB, k // 2, k % 2)
+            if t >= 5 and (t - 5) % 4 == 0 and (t - 5) // 4 < NH:
+                rs_broadcast((t - 5) // 4)
+            if 0 <= t < NS:
                 clamp_max(t, 0)
-            if 0 <= t - 1 < NS:
-                mask_sum(t - 1)
-            if t < NS:
                 clamp_max(t, 1)
                 row_scalars(t)
                 exp_row(t)
-            if t >= 7 and (t - 7) // 4 < 2 * B:
-                normalise((t - 7) // 4, (t - 7) % 4)
+            if 0 <= t + 1 < NS:
+                s_matmuls(t + 1, 0)
+            if t >= 7 and (t - 7) // 4 < NH:
+                mx_block((t - 7) // 4, (t - 7) % 4)
+            if 0 <= t + 1 < NS:
+                s_matmuls(t + 1, 1)
+            if 0 <= t - 1 < NS:
+                mask_sum(t - 1)
+                if (t - 1) % 4 == 3:
+                    rs_recip((t - 1) // 4)
+            if t >= 8 and (t - 8) // 4 < NH:
+                normalise((t - 8) // 4, (t - 8) % 4)
+            if 0 <= t < NS and t % NRB == 4:
+                f_quant(t // NRB)
+            if t >= 5 and (t - 5) % 4 == 0 and (t - 5) // 4 < NH:
+                e_quant((t - 5) // 4)

@@ -20,6 +20,7 @@ NCC = C // P
 NRB = N // P
 HALF = 512
 FLOPS = 2 * 2 * B * N * N * C
+SG_BLOCKS = (1, 3)
 
 
 def threshold_pair(t):
@@ -215,7 +216,10 @@ def tile_sapmodule_t_kernel(tc, x, threshold, out):
                     bc[:, rl * P : (rl + 1) * P], rsv[:, rl : rl + 1].to_broadcast([P, P]), ident_f[:]
                 )
             rsb = mxp.tile([P, HALF], F32, name="rsb", tag="rsb")
-            nc.scalar.copy(out=rsb[:], in_=bc[:])
+            nc.scalar.copy(
+                out=rsb[:].rearrange("p (u q e) -> p u q e", u=2, e=2),
+                in_=bc[:].rearrange("p (u e q) -> p u q e", u=2, e=2),
+            )
             st[("rsb", h)] = rsb
 
         def mx_block(h, cc):
@@ -236,12 +240,18 @@ def tile_sapmodule_t_kernel(tc, x, threshold, out):
         def normalise(h, cc):
             if cc == 0:
                 st[("osb", h)] = work.tile([P, NCC, HALF], F32, name="osb", tag="osb")
-            nc.vector.tensor_tensor(
-                out=st[("osb", h)][:, cc, :].rearrange("p (u q e) -> p u q e", u=2, e=2),
-                in0=st[("acc", h, cc)][:].rearrange("p (u e q) -> p u q e", u=2, e=2),
-                in1=st[("rsb", h)][:].rearrange("p (u e q) -> p u q e", u=2, e=2),
-                op=ALU.mult,
-            )
+            dst = st[("osb", h)][:, cc, :]
+            src = st[("acc", h, cc)][:].rearrange("p (u e q) -> p u q e", u=2, e=2)
+            if cc in SG_BLOCKS:
+                nc.scalar.copy(out=dst.rearrange("p (u q e) -> p u q e", u=2, e=2), in_=src)
+                nc.gpsimd.tensor_tensor(out=dst, in0=dst, in1=st[("rsb", h)][:], op=ALU.mult)
+            else:
+                nc.vector.tensor_tensor(
+                    out=dst.rearrange("p (u q e) -> p u q e", u=2, e=2),
+                    in0=src,
+                    in1=st[("rsb", h)][:].rearrange("p (u q e) -> p u q e", u=2, e=2),
+                    op=ALU.mult,
+                )
             b, hh = divmod(h, 2)
             if h == 2 * B - 1:
                 nc.sync.dma_start(out=ov[b][:, cc, hh * HALF : (hh + 1) * HALF], in_=st[("osb", h)][:, cc, :])
@@ -263,6 +273,8 @@ def tile_sapmodule_t_kernel(tc, x, threshold, out):
                 f_transposes(t // NRB, k // 2, k % 2)
             if t >= 5 and (t - 5) % 4 == 0 and (t - 5) // 4 < NH:
                 rs_broadcast((t - 5) // 4)
+            if t >= 8 and (t - 8) // 4 < NH and (t - 8) % 4 in SG_BLOCKS:
+                normalise((t - 8) // 4, (t - 8) % 4)
             if 0 <= t < NS:
                 clamp_max(t, 0)
                 clamp_max(t, 1)
@@ -278,7 +290,7 @@ def tile_sapmodule_t_kernel(tc, x, threshold, out):
                 mask_sum(t - 1)
                 if (t - 1) % 4 == 3:
                     rs_recip((t - 1) // 4)
-            if t >= 8 and (t - 8) // 4 < NH:
+            if t >= 8 and (t - 8) // 4 < NH and (t - 8) % 4 not in SG_BLOCKS:
                 normalise((t - 8) // 4, (t - 8) % 4)
             if 0 <= t < NS and t % NRB == 4:
                 f_quant(t // NRB)

@@ -20,7 +20,6 @@ NCC = C // P
 NRB = N // P
 HALF = 512
 FLOPS = 2 * 2 * B * N * N * C
-SG_BLOCKS = (1, 3)
 
 
 def threshold_pair(t):
@@ -61,8 +60,10 @@ def tile_sapmodule_t_kernel(tc, x, threshold, out):
             xt = xpool.tile([P, NCC, N], BF16, name="x%d" % b)
             xs.append(xt)
             if b == 0:
-                for cc in range(NCC):
-                    nc.sync.dma_start(out=xt[:, cc, :], in_=xv[b][:, cc, :])
+                for g in range(2):
+                    nc.sync.dma_start(
+                        out=xt[:, :, g * HALF : (g + 1) * HALF], in_=xv[b][:, :, g * HALF : (g + 1) * HALF]
+                    )
             else:
                 nc.sync.dma_start(out=xt[:], in_=xv[b])
 
@@ -117,7 +118,7 @@ def tile_sapmodule_t_kernel(tc, x, threshold, out):
                 out=st[("c", s)][:, g * HALF : (g + 1) * HALF],
                 in0=st[("sps", s, g)][:],
                 scalar1=t_lo,
-                scalar2=(None if g == 0 else st[("mx", s)][:, 0:1]),
+                scalar2=None,
                 op0=ALU.max,
                 op1=ALU.max,
                 accum_out=st[("mx", s)][:, g : g + 1],
@@ -126,10 +127,14 @@ def tile_sapmodule_t_kernel(tc, x, threshold, out):
         def row_scalars(s):
             mx = st[("mx", s)]
             negm = small.tile([P, 1], F32, name="negm", tag="negm")
-            nc.scalar.mul(out=negm[:], in_=mx[:, 1:2], mul=-scale)
+            nc.gpsimd.tensor_scalar(
+                out=negm[:], in0=mx[:, 0:1], scalar1=mx[:, 1:2], scalar2=-scale,
+                op0=ALU.max, op1=ALU.mult,
+            )
             thr = small.tile([P, 1], F32, name="thr", tag="thr")
             nc.gpsimd.tensor_scalar(
-                out=thr[:], in0=mx[:, 1:2], scalar1=t_hi, scalar2=None, op0=ALU.min,
+                out=thr[:], in0=mx[:, 0:1], scalar1=mx[:, 1:2], scalar2=t_hi,
+                op0=ALU.max, op1=ALU.min,
             )
             st[("negm", s)] = negm
             st[("thr", s)] = thr
@@ -216,10 +221,7 @@ def tile_sapmodule_t_kernel(tc, x, threshold, out):
                     bc[:, rl * P : (rl + 1) * P], rsv[:, rl : rl + 1].to_broadcast([P, P]), ident_f[:]
                 )
             rsb = mxp.tile([P, HALF], F32, name="rsb", tag="rsb")
-            nc.scalar.copy(
-                out=rsb[:].rearrange("p (u q e) -> p u q e", u=2, e=2),
-                in_=bc[:].rearrange("p (u e q) -> p u q e", u=2, e=2),
-            )
+            nc.scalar.copy(out=rsb[:], in_=bc[:])
             st[("rsb", h)] = rsb
 
         def mx_block(h, cc):
@@ -240,18 +242,12 @@ def tile_sapmodule_t_kernel(tc, x, threshold, out):
         def normalise(h, cc):
             if cc == 0:
                 st[("osb", h)] = work.tile([P, NCC, HALF], F32, name="osb", tag="osb")
-            dst = st[("osb", h)][:, cc, :]
-            src = st[("acc", h, cc)][:].rearrange("p (u e q) -> p u q e", u=2, e=2)
-            if cc in SG_BLOCKS:
-                nc.scalar.copy(out=dst.rearrange("p (u q e) -> p u q e", u=2, e=2), in_=src)
-                nc.gpsimd.tensor_tensor(out=dst, in0=dst, in1=st[("rsb", h)][:], op=ALU.mult)
-            else:
-                nc.vector.tensor_tensor(
-                    out=dst.rearrange("p (u q e) -> p u q e", u=2, e=2),
-                    in0=src,
-                    in1=st[("rsb", h)][:].rearrange("p (u q e) -> p u q e", u=2, e=2),
-                    op=ALU.mult,
-                )
+            nc.vector.tensor_tensor(
+                out=st[("osb", h)][:, cc, :].rearrange("p (u q e) -> p u q e", u=2, e=2),
+                in0=st[("acc", h, cc)][:].rearrange("p (u e q) -> p u q e", u=2, e=2),
+                in1=st[("rsb", h)][:].rearrange("p (u e q) -> p u q e", u=2, e=2),
+                op=ALU.mult,
+            )
             b, hh = divmod(h, 2)
             if h == 2 * B - 1:
                 nc.sync.dma_start(out=ov[b][:, cc, hh * HALF : (hh + 1) * HALF], in_=st[("osb", h)][:, cc, :])
@@ -261,7 +257,7 @@ def tile_sapmodule_t_kernel(tc, x, threshold, out):
         NS = B * NRB
         NH = 2 * B
         ctx.enter_context(tc.manual_schedule())
-        for t in range(-1, NS + 9):
+        for t in range(-1, NS + 2):
             if 0 <= t < NS:
                 s_mirror(t, 0)
                 s_mirror(t, 1)
@@ -273,8 +269,6 @@ def tile_sapmodule_t_kernel(tc, x, threshold, out):
                 f_transposes(t // NRB, k // 2, k % 2)
             if t >= 5 and (t - 5) % 4 == 0 and (t - 5) // 4 < NH:
                 rs_broadcast((t - 5) // 4)
-            if t >= 8 and (t - 8) // 4 < NH and (t - 8) % 4 in SG_BLOCKS:
-                normalise((t - 8) // 4, (t - 8) % 4)
             if 0 <= t < NS:
                 clamp_max(t, 0)
                 clamp_max(t, 1)
@@ -288,11 +282,20 @@ def tile_sapmodule_t_kernel(tc, x, threshold, out):
                 s_matmuls(t + 1, 1)
             if 0 <= t - 1 < NS:
                 mask_sum(t - 1)
-                if (t - 1) % 4 == 3:
-                    rs_recip((t - 1) // 4)
-            if t >= 8 and (t - 8) // 4 < NH and (t - 8) % 4 not in SG_BLOCKS:
+            if t >= 8 and (t - 8) // 4 < NH:
                 normalise((t - 8) // 4, (t - 8) % 4)
+            if 0 <= t - 1 < NS and (t - 1) % 4 == 3:
+                rs_recip((t - 1) // 4)
             if 0 <= t < NS and t % NRB == 4:
                 f_quant(t // NRB)
-            if t >= 5 and (t - 5) % 4 == 0 and (t - 5) // 4 < NH:
+            if t >= 5 and (t - 5) % 4 == 0 and (t - 5) // 4 < NH - 1:
                 e_quant((t - 5) // 4)
+        mx_block(NH - 2, 3)
+        normalise(NH - 2, 2)
+        normalise(NH - 2, 3)
+        e_quant(NH - 1)
+        mx_block(NH - 1, 0)
+        for cc in range(1, NCC):
+            mx_block(NH - 1, cc)
+            normalise(NH - 1, cc - 1)
+        normalise(NH - 1, NCC - 1)

@@ -76,26 +76,17 @@ def tile_sapmodule_t_kernel(tc, x, threshold, out):
 
         def s_matmuls(s, g):
             b, r = divmod(s, NRB)
-            xp = xs[b][:].rearrange("p cc (r q e) -> p cc r e q", q=P, e=2)
+            xt = xs[b]
             sps = ps_s.tile([P, HALF], F32, name="sps", tag="sps")
             st[("sps", s, g)] = sps
             k_first = max(r - 4 * g, 0)
             groups = {0: [(0, 4)], 1: [(1, 2), (2, 4)], 2: [(2, 4)], 3: [(3, 4)]}.get(k_first, [])
             for k0, k1 in groups:
                 for cc in range(NCC):
-                    if k1 - k0 == 4:
-                        rhs = xp[:, cc, 2 * g : 2 * g + 2, :, :]
-                        dst = sps[:].rearrange("p (u e q) -> p u e q", u=2, e=2)
-                    elif k1 - k0 == 2:
-                        rhs = xp[:, cc, 2 * g + 1, :, :]
-                        dst = sps[:, k0 * P : k1 * P].rearrange("p (e q) -> p e q", e=2)
-                    else:
-                        rhs = xp[:, cc, 2 * g + k0 // 2, 1, :]
-                        dst = sps[:, k0 * P : k1 * P]
                     nc.tensor.matmul(
-                        out=dst,
-                        lhsT=xp[:, cc, r // 2, r % 2, :],
-                        rhs=rhs,
+                        out=sps[:, k0 * P : k1 * P],
+                        lhsT=xt[:, cc, r * P : (r + 1) * P],
+                        rhs=xt[:, cc, g * HALF + k0 * P : g * HALF + k1 * P],
                         start=(cc == 0),
                         stop=(cc == NCC - 1),
                     )
@@ -186,25 +177,22 @@ def tile_sapmodule_t_kernel(tc, x, threshold, out):
             st[("esc", h)] = esc
 
         def f_transposes(b, g, cp):
-            xw = xs[b][:].rearrange("p cc n -> p (cc n)").bitcast(F32)
-            ft = ps_t.tile([P, 2, 2 * P], F32, name="ft", tag="tp")
-            for u in range(2):
-                for c2 in range(2):
-                    cc = 2 * cp + c2
-                    w0 = cc * (N // 2) + (2 * g + u) * P
-                    nc.tensor.transpose(ft[:, u, c2 * P : (c2 + 1) * P], xw[:, w0 : w0 + P], ident_f[:])
+            ft = ps_t.tile([P, 2, 4, P], BF16, name="ft", tag="tp")
+            for c2 in range(2):
+                for t4 in range(4):
+                    j0 = g * HALF + t4 * P
+                    nc.tensor.transpose(ft[:, c2, t4, :], xs[b][:, 2 * cp + c2, j0 : j0 + P], ident_bf[:])
             if g == 0 and cp == 0:
-                st[("fgrp", b)] = mxp.tile([P, 4 * N], BF16, name="fgrp", tag="fgrp", align_bytes=64)
-            fgw = st[("fgrp", b)][:].bitcast(F32).rearrange("p (g c u) -> p g c u", g=2, u=2)
+                st[("fgrp", b)] = mxp.tile([P, 2, NCC, P, 4], BF16, name="fgrp", tag="fgrp", align_bytes=64)
             nc.scalar.copy(
-                out=fgw[:, g, cp * 2 * P : (cp + 1) * 2 * P, :],
-                in_=ft[:].rearrange("p u c -> p c u"),
+                out=st[("fgrp", b)][:, g, 2 * cp : 2 * cp + 2, :, :],
+                in_=ft[:].rearrange("p a t c -> p a c t"),
             )
 
         def f_quant(b):
             fcod = mxp.tile([P, 2 * C], U32, name="fcod", tag="fcod", align_bytes=64)
             fsc = mxp.tile([P, 2 * C], U8, name="fsc", tag="fsc", align_bytes=64)
-            nc.vector.quantize_mx(out=fcod[:].bitcast(FP8X4), scales=fsc[:], in_=st[("fgrp", b)][:])
+            nc.vector.quantize_mx(out=fcod[:].bitcast(FP8X4), scales=fsc[:], in_=st[("fgrp", b)][:].rearrange("p g a c t -> p (g a c t)"))
             st[("fcod", b)] = fcod
             st[("fsc", b)] = fsc
 
@@ -243,10 +231,7 @@ def tile_sapmodule_t_kernel(tc, x, threshold, out):
             if cc == 0:
                 st[("osb", h)] = work.tile([P, NCC, HALF], F32, name="osb", tag="osb")
             nc.vector.tensor_tensor(
-                out=st[("osb", h)][:, cc, :].rearrange("p (u q e) -> p u q e", u=2, e=2),
-                in0=st[("acc", h, cc)][:].rearrange("p (u e q) -> p u q e", u=2, e=2),
-                in1=st[("rsb", h)][:].rearrange("p (u e q) -> p u q e", u=2, e=2),
-                op=ALU.mult,
+                out=st[("osb", h)][:, cc, :], in0=st[("acc", h, cc)][:], in1=st[("rsb", h)][:], op=ALU.mult
             )
             b, hh = divmod(h, 2)
             if h == 2 * B - 1:

@@ -20,6 +20,7 @@ NCC = C // P
 NRB = N // P
 HALF = 512
 FLOPS = 2 * 2 * B * N * N * C
+SG_BLOCKS = (1, 3)
 
 
 def threshold_pair(t):
@@ -76,17 +77,26 @@ def tile_sapmodule_t_kernel(tc, x, threshold, out):
 
         def s_matmuls(s, g):
             b, r = divmod(s, NRB)
-            xt = xs[b]
+            xp = xs[b][:].rearrange("p cc (r q e) -> p cc r e q", q=P, e=2)
             sps = ps_s.tile([P, HALF], F32, name="sps", tag="sps")
             st[("sps", s, g)] = sps
             k_first = max(r - 4 * g, 0)
             groups = {0: [(0, 4)], 1: [(1, 2), (2, 4)], 2: [(2, 4)], 3: [(3, 4)]}.get(k_first, [])
             for k0, k1 in groups:
                 for cc in range(NCC):
+                    if k1 - k0 == 4:
+                        rhs = xp[:, cc, 2 * g : 2 * g + 2, :, :]
+                        dst = sps[:].rearrange("p (u e q) -> p u e q", u=2, e=2)
+                    elif k1 - k0 == 2:
+                        rhs = xp[:, cc, 2 * g + 1, :, :]
+                        dst = sps[:, k0 * P : k1 * P].rearrange("p (e q) -> p e q", e=2)
+                    else:
+                        rhs = xp[:, cc, 2 * g + k0 // 2, 1, :]
+                        dst = sps[:, k0 * P : k1 * P]
                     nc.tensor.matmul(
-                        out=sps[:, k0 * P : k1 * P],
-                        lhsT=xt[:, cc, r * P : (r + 1) * P],
-                        rhs=xt[:, cc, g * HALF + k0 * P : g * HALF + k1 * P],
+                        out=dst,
+                        lhsT=xp[:, cc, r // 2, r % 2, :],
+                        rhs=rhs,
                         start=(cc == 0),
                         stop=(cc == NCC - 1),
                     )
@@ -177,22 +187,25 @@ def tile_sapmodule_t_kernel(tc, x, threshold, out):
             st[("esc", h)] = esc
 
         def f_transposes(b, g, cp):
-            ft = ps_t.tile([P, 2, 4, P], BF16, name="ft", tag="tp")
-            for c2 in range(2):
-                for t4 in range(4):
-                    j0 = g * HALF + t4 * P
-                    nc.tensor.transpose(ft[:, c2, t4, :], xs[b][:, 2 * cp + c2, j0 : j0 + P], ident_bf[:])
+            xw = xs[b][:].rearrange("p cc n -> p (cc n)").bitcast(F32)
+            ft = ps_t.tile([P, 2, 2 * P], F32, name="ft", tag="tp")
+            for u in range(2):
+                for c2 in range(2):
+                    cc = 2 * cp + c2
+                    w0 = cc * (N // 2) + (2 * g + u) * P
+                    nc.tensor.transpose(ft[:, u, c2 * P : (c2 + 1) * P], xw[:, w0 : w0 + P], ident_f[:])
             if g == 0 and cp == 0:
-                st[("fgrp", b)] = mxp.tile([P, 2, NCC, P, 4], BF16, name="fgrp", tag="fgrp", align_bytes=64)
+                st[("fgrp", b)] = mxp.tile([P, 4 * N], BF16, name="fgrp", tag="fgrp", align_bytes=64)
+            fgw = st[("fgrp", b)][:].bitcast(F32).rearrange("p (g c u) -> p g c u", g=2, u=2)
             nc.scalar.copy(
-                out=st[("fgrp", b)][:, g, 2 * cp : 2 * cp + 2, :, :],
-                in_=ft[:].rearrange("p a t c -> p a c t"),
+                out=fgw[:, g, cp * 2 * P : (cp + 1) * 2 * P, :],
+                in_=ft[:].rearrange("p u c -> p c u"),
             )
 
         def f_quant(b):
             fcod = mxp.tile([P, 2 * C], U32, name="fcod", tag="fcod", align_bytes=64)
             fsc = mxp.tile([P, 2 * C], U8, name="fsc", tag="fsc", align_bytes=64)
-            nc.vector.quantize_mx(out=fcod[:].bitcast(FP8X4), scales=fsc[:], in_=st[("fgrp", b)][:].rearrange("p g a c t -> p (g a c t)"))
+            nc.vector.quantize_mx(out=fcod[:].bitcast(FP8X4), scales=fsc[:], in_=st[("fgrp", b)][:])
             st[("fcod", b)] = fcod
             st[("fsc", b)] = fsc
 
@@ -209,7 +222,10 @@ def tile_sapmodule_t_kernel(tc, x, threshold, out):
                     bc[:, rl * P : (rl + 1) * P], rsv[:, rl : rl + 1].to_broadcast([P, P]), ident_f[:]
                 )
             rsb = mxp.tile([P, HALF], F32, name="rsb", tag="rsb")
-            nc.scalar.copy(out=rsb[:], in_=bc[:])
+            nc.scalar.copy(
+                out=rsb[:].rearrange("p (u q e) -> p u q e", u=2, e=2),
+                in_=bc[:].rearrange("p (u e q) -> p u q e", u=2, e=2),
+            )
             st[("rsb", h)] = rsb
 
         def mx_block(h, cc):
@@ -230,9 +246,18 @@ def tile_sapmodule_t_kernel(tc, x, threshold, out):
         def normalise(h, cc):
             if cc == 0:
                 st[("osb", h)] = work.tile([P, NCC, HALF], F32, name="osb", tag="osb")
-            nc.vector.tensor_tensor(
-                out=st[("osb", h)][:, cc, :], in0=st[("acc", h, cc)][:], in1=st[("rsb", h)][:], op=ALU.mult
-            )
+            dst = st[("osb", h)][:, cc, :]
+            src = st[("acc", h, cc)][:].rearrange("p (u e q) -> p u q e", u=2, e=2)
+            if cc in SG_BLOCKS and h < 2 * B - 1:
+                nc.scalar.copy(out=dst.rearrange("p (u q e) -> p u q e", u=2, e=2), in_=src)
+                nc.gpsimd.tensor_tensor(out=dst, in0=dst, in1=st[("rsb", h)][:], op=ALU.mult)
+            else:
+                nc.vector.tensor_tensor(
+                    out=dst.rearrange("p (u q e) -> p u q e", u=2, e=2),
+                    in0=src,
+                    in1=st[("rsb", h)][:].rearrange("p (u q e) -> p u q e", u=2, e=2),
+                    op=ALU.mult,
+                )
             b, hh = divmod(h, 2)
             if h == 2 * B - 1:
                 nc.sync.dma_start(out=ov[b][:, cc, hh * HALF : (hh + 1) * HALF], in_=st[("osb", h)][:, cc, :])
@@ -258,6 +283,9 @@ def tile_sapmodule_t_kernel(tc, x, threshold, out):
                 clamp_max(t, 0)
                 clamp_max(t, 1)
                 row_scalars(t)
+            if t >= 8 and (t - 8) // 4 < NH and (t - 8) % 4 in SG_BLOCKS:
+                normalise((t - 8) // 4, (t - 8) % 4)
+            if 0 <= t < NS:
                 exp_row(t)
             if 0 <= t + 1 < NS:
                 s_matmuls(t + 1, 0)
@@ -267,7 +295,7 @@ def tile_sapmodule_t_kernel(tc, x, threshold, out):
                 s_matmuls(t + 1, 1)
             if 0 <= t - 1 < NS:
                 mask_sum(t - 1)
-            if t >= 8 and (t - 8) // 4 < NH:
+            if t >= 8 and (t - 8) // 4 < NH and (t - 8) % 4 not in SG_BLOCKS:
                 normalise((t - 8) // 4, (t - 8) % 4)
             if 0 <= t - 1 < NS and (t - 1) % 4 == 3:
                 rs_recip((t - 1) // 4)

@@ -152,7 +152,7 @@ def tile_sapmodule_t_kernel(tc, x, threshold, out):
             h, rl = divmod(s, 4)
             if rl == 0:
                 st[("ssum", h)] = small.tile([P, 4], F32, name="ssum", tag="ssum")
-            ebf = work.tile([P, N], BF16, name="ebf", tag="ebf")
+            ebf = work.tile([P, N], BF16, name="ebf", tag="ebf", bufs=4)
             nc.vector.scalar_tensor_tensor(
                 out=ebf[:], in0=st[("c", s)][:], scalar=st[("thr", s)][:, 0:1],
                 in1=st[("e2", s)][:], op0=ALU.is_ge, op1=ALU.mult,
@@ -267,13 +267,13 @@ def tile_sapmodule_t_kernel(tc, x, threshold, out):
         NS = B * NRB
         NH = 2 * B
         ctx.enter_context(tc.manual_schedule())
-        for t in range(-1, NS + 2):
+        for t in range(-1, NS + 3):
             if 0 <= t < NS:
                 s_mirror(t, 0)
                 s_mirror(t, 1)
-            if 0 <= t - 2 < NS:
-                e_transposes(t - 2)
-                e_regroup(t - 2)
+            if 0 <= t - 3 < NS:
+                e_transposes(t - 3)
+                e_regroup(t - 3)
             if 0 <= t < NS and t % NRB in (0, 2, 3, 4):
                 k = (0, 2, 3, 4).index(t % NRB)
                 f_transposes(t // NRB, k // 2, k % 2)
@@ -283,26 +283,26 @@ def tile_sapmodule_t_kernel(tc, x, threshold, out):
                 clamp_max(t, 0)
                 clamp_max(t, 1)
                 row_scalars(t)
-            if t >= 8 and (t - 8) // 4 < NH and (t - 8) % 4 in SG_BLOCKS:
-                normalise((t - 8) // 4, (t - 8) % 4)
+            if t >= 9 and (t - 9) // 4 < NH and (t - 9) % 4 in SG_BLOCKS:
+                normalise((t - 9) // 4, (t - 9) % 4)
             if 0 <= t < NS:
                 exp_row(t)
             if 0 <= t + 1 < NS:
                 s_matmuls(t + 1, 0)
-            if t >= 7 and (t - 7) // 4 < NH:
-                mx_block((t - 7) // 4, (t - 7) % 4)
+            if t >= 8 and (t - 8) // 4 < NH:
+                mx_block((t - 8) // 4, (t - 8) % 4)
             if 0 <= t + 1 < NS:
                 s_matmuls(t + 1, 1)
             if 0 <= t - 1 < NS:
                 mask_sum(t - 1)
-            if t >= 8 and (t - 8) // 4 < NH and (t - 8) % 4 not in SG_BLOCKS:
-                normalise((t - 8) // 4, (t - 8) % 4)
+            if t >= 9 and (t - 9) // 4 < NH and (t - 9) % 4 not in SG_BLOCKS:
+                normalise((t - 9) // 4, (t - 9) % 4)
             if 0 <= t - 1 < NS and (t - 1) % 4 == 3:
                 rs_recip((t - 1) // 4)
             if 0 <= t < NS and t % NRB == 4:
                 f_quant(t // NRB)
-            if t >= 5 and (t - 5) % 4 == 0 and (t - 5) // 4 < NH - 1:
-                e_quant((t - 5) // 4)
+            if t >= 6 and (t - 6) % 4 == 0 and (t - 6) // 4 < NH - 1:
+                e_quant((t - 6) // 4)
         mx_block(NH - 2, 3)
         normalise(NH - 2, 2)
         normalise(NH - 2, 3)

@@ -21,6 +21,7 @@ NRB = N // P
 HALF = 512
 FLOPS = 2 * 2 * B * N * N * C
 SG_BLOCKS = (1, 3)
+STEEP = 2.0 ** 40
 
 
 def threshold_pair(t):
@@ -40,7 +41,7 @@ def tile_sapmodule_t_kernel(tc, x, threshold, out):
     nc = tc.nc
     assert threshold > 0.0
     scale = 1.0 / math.sqrt(C)
-    t_lo, t_hi = threshold_pair(threshold * math.sqrt(C))
+    t_hi = threshold_pair(threshold * math.sqrt(C))[1]
 
     xv = x.rearrange("b (p cc) h w -> b p cc (h w)", cc=NCC)
     ov = out.rearrange("b (m cc) h w -> b m cc (h w)", cc=NCC)
@@ -68,8 +69,6 @@ def tile_sapmodule_t_kernel(tc, x, threshold, out):
             else:
                 nc.sync.dma_start(out=xt[:], in_=xv[b])
 
-        ident_bf = const.tile([P, P], BF16, name="ident_bf")
-        make_identity(nc, ident_bf[:])
         ident_f = const.tile([P, P], F32, name="ident_f")
         make_identity(nc, ident_f[:])
 
@@ -77,26 +76,16 @@ def tile_sapmodule_t_kernel(tc, x, threshold, out):
 
         def s_matmuls(s, g):
             b, r = divmod(s, NRB)
-            xp = xs[b][:].rearrange("p cc (r q e) -> p cc r e q", q=P, e=2)
             sps = ps_s.tile([P, HALF], F32, name="sps", tag="sps")
             st[("sps", s, g)] = sps
             k_first = max(r - 4 * g, 0)
-            groups = {0: [(0, 4)], 1: [(1, 2), (2, 4)], 2: [(2, 4)], 3: [(3, 4)]}.get(k_first, [])
+            groups = [(k_first, 4)] if k_first < 4 else []
             for k0, k1 in groups:
                 for cc in range(NCC):
-                    if k1 - k0 == 4:
-                        rhs = xp[:, cc, 2 * g : 2 * g + 2, :, :]
-                        dst = sps[:].rearrange("p (u e q) -> p u e q", u=2, e=2)
-                    elif k1 - k0 == 2:
-                        rhs = xp[:, cc, 2 * g + 1, :, :]
-                        dst = sps[:, k0 * P : k1 * P].rearrange("p (e q) -> p e q", e=2)
-                    else:
-                        rhs = xp[:, cc, 2 * g + k0 // 2, 1, :]
-                        dst = sps[:, k0 * P : k1 * P]
                     nc.tensor.matmul(
-                        out=dst,
-                        lhsT=xp[:, cc, r // 2, r % 2, :],
-                        rhs=rhs,
+                        out=sps[:, k0 * P : k1 * P],
+                        lhsT=xs[b][:, cc, r * P : (r + 1) * P],
+                        rhs=xs[b][:, cc, g * HALF + k0 * P : g * HALF + k1 * P],
                         start=(cc == 0),
                         stop=(cc == NCC - 1),
                     )
@@ -107,73 +96,87 @@ def tile_sapmodule_t_kernel(tc, x, threshold, out):
             for k in range(min(max(r - 4 * g, 0), 4)):
                 nc.tensor.transpose(
                     sps[:, k * P : (k + 1) * P],
-                    st[("c", b * NRB + 4 * g + k)][:, r * P : (r + 1) * P],
+                    st[("z", b * NRB + 4 * g + k)][:, r * P : (r + 1) * P],
                     ident_f[:],
                 )
 
-        def clamp_max(s, g):
+        def exit_max(s, g):
+            r = s % NRB
             if g == 0:
-                st[("c", s)] = clp.tile([P, N], F32, name="cl", tag="cl")
-                st[("mx", s)] = small.tile([P, 2], F32, name="mx", tag="mx")
-            nc.vector.tensor_scalar(
-                out=st[("c", s)][:, g * HALF : (g + 1) * HALF],
-                in0=st[("sps", s, g)][:],
-                scalar1=t_lo,
-                scalar2=None,
-                op0=ALU.max,
-                op1=ALU.max,
-                accum_out=st[("mx", s)][:, g : g + 1],
+                st[("z", s)] = clp.tile([P, N], F32, name="z", tag="z")
+                st[("d", s)] = work.tile([P, N], F32, name="d", tag="d")
+                st[("mx", s)] = small.tile([P, 4], F32, name="mx", tag="mx")
+                st[("parts", s)] = []
+            split = min(max(r - 4 * g, 0), 4) * P
+            for lo, hi in ((split, HALF), (0, split)):
+                if lo == hi:
+                    continue
+                j = len(st[("parts", s)])
+                st[("parts", s)].append(j)
+                direct = hi == HALF and lo == split and split < HALF
+                nc.vector.tensor_scalar(
+                    out=st[("d" if direct else "z", s)][:, g * HALF + lo : g * HALF + hi],
+                    in0=st[("sps", s, g)][:, lo:hi],
+                    scalar1=t_hi if direct else 1.0,
+                    scalar2=None,
+                    op0=ALU.subtract if direct else ALU.mult,
+                    op1=ALU.max,
+                    accum_out=st[("mx", s)][:, j : j + 1],
+                )
+
+        def steep_mask(s):
+            r = s % NRB
+            d = st[("d", s)][:, r * P :]
+            nc.vector.scalar_tensor_tensor(
+                out=st[("z", s)][:, r * P :], in0=d, scalar=STEEP, in1=d, op0=ALU.mult, op1=ALU.min
             )
 
         def row_scalars(s):
             mx = st[("mx", s)]
+            last = len(st[("parts", s)]) - 1
+            m = small.tile([P, 1], F32, name="m", tag="m")
+            nc.gpsimd.tensor_scalar(
+                out=m[:], in0=mx[:, 0:1], scalar1=mx[:, 1:2], scalar2=mx[:, last : last + 1],
+                op0=ALU.max, op1=ALU.max,
+            )
             negm = small.tile([P, 1], F32, name="negm", tag="negm")
             nc.gpsimd.tensor_scalar(
-                out=negm[:], in0=mx[:, 0:1], scalar1=mx[:, 1:2], scalar2=-scale,
-                op0=ALU.max, op1=ALU.mult,
+                out=negm[:], in0=m[:], scalar1=0.0, scalar2=-scale, op0=ALU.max, op1=ALU.mult
             )
-            thr = small.tile([P, 1], F32, name="thr", tag="thr")
+            rsc = small.tile([P, 1], F32, name="rsc", tag="rsc")
             nc.gpsimd.tensor_scalar(
-                out=thr[:], in0=mx[:, 0:1], scalar1=mx[:, 1:2], scalar2=t_hi,
-                op0=ALU.max, op1=ALU.min,
+                out=rsc[:], in0=m[:], scalar1=0.0, scalar2=scale, op0=ALU.is_ge, op1=ALU.mult
             )
             st[("negm", s)] = negm
-            st[("thr", s)] = thr
+            st[("rsc", s)] = rsc
 
         def exp_row(s):
-            e2 = work.tile([P, N], F32, name="e2", tag="e2")
-            nc.scalar.activation(
-                out=e2[:], in_=st[("c", s)][:], func=ACT.Exp,
-                bias=st[("negm", s)][:, 0:1], scale=scale,
-            )
-            st[("e2", s)] = e2
-
-        def mask_sum(s):
             h, rl = divmod(s, 4)
             if rl == 0:
                 st[("ssum", h)] = small.tile([P, 4], F32, name="ssum", tag="ssum")
             ebf = work.tile([P, N], BF16, name="ebf", tag="ebf", bufs=4)
-            nc.vector.scalar_tensor_tensor(
-                out=ebf[:], in0=st[("c", s)][:], scalar=st[("thr", s)][:, 0:1],
-                in1=st[("e2", s)][:], op0=ALU.is_ge, op1=ALU.mult,
+            nc.scalar.activation(
+                out=ebf[:], in_=st[("z", s)][:], func=ACT.Exp,
+                bias=st[("negm", s)][:, 0:1], scale=st[("rsc", s)][:, 0:1],
                 accum_out=st[("ssum", h)][:, rl : rl + 1],
             )
             st[("ebf", s)] = ebf
 
         def e_transposes(s):
-            tp = ps_t.tile([P, NRB, P], BF16, name="tp", tag="tp")
-            ebf = st[("ebf", s)]
-            for k in range(NRB):
-                nc.tensor.transpose(tp[:, k, :], ebf[:, k * P : (k + 1) * P], ident_bf[:])
+            tp = ps_t.tile([P, NRB // 2, P], F32, name="tp", tag="tp")
+            ew = st[("ebf", s)][:].bitcast(F32)
+            for k in range(NRB // 2):
+                nc.tensor.transpose(tp[:, k, :], ew[:, k * P : (k + 1) * P], ident_f[:])
             st[("tp", s)] = tp
 
         def e_regroup(s):
             h, rl = divmod(s, 4)
             if rl == 0:
-                st[("grp", h)] = mxp.tile([P, 2, HALF, 4], BF16, name="grp", tag="grp", align_bytes=64)
+                st[("grp", h)] = mxp.tile([P, 8 * HALF], BF16, name="grp", tag="grp", align_bytes=64)
+            gw = st[("grp", h)][:].bitcast(F32).rearrange("p (g i u) -> p g i u", g=2, u=2)
             nc.scalar.copy(
-                out=st[("grp", h)][:, :, rl * P : (rl + 1) * P, :],
-                in_=st[("tp", s)][:].rearrange("p (g t) i -> p g i t", g=2),
+                out=gw[:, :, rl * P : (rl + 1) * P, :],
+                in_=st[("tp", s)][:].rearrange("p (g u) i -> p g i u", g=2),
             )
 
         def e_quant(h):
@@ -181,7 +184,7 @@ def tile_sapmodule_t_kernel(tc, x, threshold, out):
             esc = mxp.tile([P, 2 * HALF], U8, name="esc", tag="esc", align_bytes=64)
             nc.vector.quantize_mx(
                 out=ecod[:].bitcast(FP8X4), scales=esc[:],
-                in_=st[("grp", h)][:].rearrange("p g n t -> p (g n t)"),
+                in_=st[("grp", h)][:],
             )
             st[("ecod", h)] = ecod
             st[("esc", h)] = esc
@@ -222,10 +225,7 @@ def tile_sapmodule_t_kernel(tc, x, threshold, out):
                     bc[:, rl * P : (rl + 1) * P], rsv[:, rl : rl + 1].to_broadcast([P, P]), ident_f[:]
                 )
             rsb = mxp.tile([P, HALF], F32, name="rsb", tag="rsb")
-            nc.scalar.copy(
-                out=rsb[:].rearrange("p (u q e) -> p u q e", u=2, e=2),
-                in_=bc[:].rearrange("p (u e q) -> p u q e", u=2, e=2),
-            )
+            nc.scalar.copy(out=rsb[:], in_=bc[:])
             st[("rsb", h)] = rsb
 
         def mx_block(h, cc):
@@ -247,17 +247,12 @@ def tile_sapmodule_t_kernel(tc, x, threshold, out):
             if cc == 0:
                 st[("osb", h)] = work.tile([P, NCC, HALF], F32, name="osb", tag="osb")
             dst = st[("osb", h)][:, cc, :]
-            src = st[("acc", h, cc)][:].rearrange("p (u e q) -> p u q e", u=2, e=2)
+            src = st[("acc", h, cc)][:]
             if cc in SG_BLOCKS and h < 2 * B - 1:
-                nc.scalar.copy(out=dst.rearrange("p (u q e) -> p u q e", u=2, e=2), in_=src)
+                nc.scalar.copy(out=dst, in_=src)
                 nc.gpsimd.tensor_tensor(out=dst, in0=dst, in1=st[("rsb", h)][:], op=ALU.mult)
             else:
-                nc.vector.tensor_tensor(
-                    out=dst.rearrange("p (u q e) -> p u q e", u=2, e=2),
-                    in0=src,
-                    in1=st[("rsb", h)][:].rearrange("p (u q e) -> p u q e", u=2, e=2),
-                    op=ALU.mult,
-                )
+                nc.vector.tensor_tensor(out=dst, in0=src, in1=st[("rsb", h)][:], op=ALU.mult)
             b, hh = divmod(h, 2)
             if h == 2 * B - 1:
                 nc.sync.dma_start(out=ov[b][:, cc, hh * HALF : (hh + 1) * HALF], in_=st[("osb", h)][:, cc, :])
@@ -267,42 +262,41 @@ def tile_sapmodule_t_kernel(tc, x, threshold, out):
         NS = B * NRB
         NH = 2 * B
         ctx.enter_context(tc.manual_schedule())
-        for t in range(-1, NS + 3):
+        for t in range(-1, NS + 2):
             if 0 <= t < NS:
                 s_mirror(t, 0)
                 s_mirror(t, 1)
-            if 0 <= t - 3 < NS:
-                e_transposes(t - 3)
-                e_regroup(t - 3)
+            if 0 <= t - 2 < NS:
+                e_transposes(t - 2)
+                e_regroup(t - 2)
             if 0 <= t < NS and t % NRB in (0, 2, 3, 4):
                 k = (0, 2, 3, 4).index(t % NRB)
                 f_transposes(t // NRB, k // 2, k % 2)
             if t >= 5 and (t - 5) % 4 == 0 and (t - 5) // 4 < NH:
                 rs_broadcast((t - 5) // 4)
             if 0 <= t < NS:
-                clamp_max(t, 0)
-                clamp_max(t, 1)
+                exit_max(t, 0)
+                exit_max(t, 1)
                 row_scalars(t)
-            if t >= 9 and (t - 9) // 4 < NH and (t - 9) % 4 in SG_BLOCKS:
-                normalise((t - 9) // 4, (t - 9) % 4)
+                steep_mask(t)
+            if t >= 8 and (t - 8) // 4 < NH and (t - 8) % 4 in SG_BLOCKS:
+                normalise((t - 8) // 4, (t - 8) % 4)
             if 0 <= t < NS:
                 exp_row(t)
             if 0 <= t + 1 < NS:
                 s_matmuls(t + 1, 0)
-            if t >= 8 and (t - 8) // 4 < NH:
-                mx_block((t - 8) // 4, (t - 8) % 4)
+            if t >= 7 and (t - 7) // 4 < NH:
+                mx_block((t - 7) // 4, (t - 7) % 4)
             if 0 <= t + 1 < NS:
                 s_matmuls(t + 1, 1)
-            if 0 <= t - 1 < NS:
-                mask_sum(t - 1)
-            if t >= 9 and (t - 9) // 4 < NH and (t - 9) % 4 not in SG_BLOCKS:
-                normalise((t - 9) // 4, (t - 9) % 4)
+            if t >= 8 and (t - 8) // 4 < NH and (t - 8) % 4 not in SG_BLOCKS:
+                normalise((t - 8) // 4, (t - 8) % 4)
             if 0 <= t - 1 < NS and (t - 1) % 4 == 3:
                 rs_recip((t - 1) // 4)
             if 0 <= t < NS and t % NRB == 4:
                 f_quant(t // NRB)
-            if t >= 6 and (t - 6) % 4 == 0 and (t - 6) // 4 < NH - 1:
-                e_quant((t - 6) // 4)
+            if t >= 5 and (t - 5) % 4 == 0 and (t - 5) // 4 < NH - 1:
+                e_quant((t - 5) // 4)
         mx_block(NH - 2, 3)
         normalise(NH - 2, 2)
         normalise(NH - 2, 3)

@@ -20,7 +20,7 @@ NCC = C // P
 NRB = N // P
 HALF = 512
 FLOPS = 2 * 2 * B * N * N * C
-SG_BLOCKS = (1, 3)
+SG_BLOCKS = (0, 1, 3)
 STEEP = 2.0 ** 40
 
 
@@ -74,54 +74,63 @@ def tile_sapmodule_t_kernel(tc, x, threshold, out):
 
         st = {}
 
-        def s_matmuls(s, g):
-            b, r = divmod(s, NRB)
-            sps = ps_s.tile([P, HALF], F32, name="sps", tag="sps")
-            st[("sps", s, g)] = sps
-            k_first = max(r - 4 * g, 0)
-            groups = [(k_first, 4)] if k_first < 4 else []
-            for k0, k1 in groups:
-                for cc in range(NCC):
-                    nc.tensor.matmul(
-                        out=sps[:, k0 * P : k1 * P],
-                        lhsT=xs[b][:, cc, r * P : (r + 1) * P],
-                        rhs=xs[b][:, cc, g * HALF + k0 * P : g * HALF + k1 * P],
-                        start=(cc == 0),
-                        stop=(cc == NCC - 1),
-                    )
+        def bank_runs(n_blocks):
+            return [(k, min(k + 4, n_blocks)) for k in range(0, n_blocks, 4)]
 
-        def s_mirror(s, g):
+        def s_matmuls(s, i):
             b, r = divmod(s, NRB)
-            sps = st[("sps", s, g)]
-            for k in range(min(max(r - 4 * g, 0), 4)):
-                nc.tensor.transpose(
-                    sps[:, k * P : (k + 1) * P],
-                    st[("z", b * NRB + 4 * g + k)][:, r * P : (r + 1) * P],
-                    ident_f[:],
+            runs = bank_runs(NRB - r)
+            if i >= len(runs):
+                return
+            k0, k1 = runs[i]
+            sps = ps_s.tile([P, HALF], F32, name="sps", tag="sps")
+            st[("sps", s, i)] = sps
+            for cc in range(NCC):
+                nc.tensor.matmul(
+                    out=sps[:, : (k1 - k0) * P],
+                    lhsT=xs[b][:, cc, r * P : (r + 1) * P],
+                    rhs=xs[b][:, cc, (r + k0) * P : (r + k1) * P],
+                    start=(cc == 0),
+                    stop=(cc == NCC - 1),
                 )
 
-        def exit_max(s, g):
+        def s_mirror(s):
+            b, r = divmod(s, NRB)
+            for k0, k1 in bank_runs(r):
+                spm = ps_s.tile([P, HALF], F32, name="spm", tag="sps")
+                st[("spm", s, k0)] = spm
+                for k in range(k0, k1):
+                    nc.tensor.transpose(
+                        spm[:, (k - k0) * P : (k - k0 + 1) * P],
+                        st[("z", b * NRB + k)][:, r * P : (r + 1) * P],
+                        ident_f[:],
+                    )
+
+        def exit_max(s, out, in_, op0, scalar1):
+            j = st[("nmx", s)]
+            st[("nmx", s)] = j + 1
+            nc.vector.tensor_scalar(
+                out=out, in0=in_, scalar1=scalar1, scalar2=None, op0=op0, op1=ALU.max,
+                accum_out=st[("mx", s)][:, j : j + 1],
+            )
+
+        def exit_direct(s):
             r = s % NRB
-            if g == 0:
-                st[("z", s)] = clp.tile([P, N], F32, name="z", tag="z")
-                st[("d", s)] = work.tile([P, N], F32, name="d", tag="d")
-                st[("mx", s)] = small.tile([P, 4], F32, name="mx", tag="mx")
-                st[("parts", s)] = []
-            split = min(max(r - 4 * g, 0), 4) * P
-            for lo, hi in ((split, HALF), (0, split)):
-                if lo == hi:
-                    continue
-                j = len(st[("parts", s)])
-                st[("parts", s)].append(j)
-                direct = hi == HALF and lo == split and split < HALF
-                nc.vector.tensor_scalar(
-                    out=st[("d" if direct else "z", s)][:, g * HALF + lo : g * HALF + hi],
-                    in0=st[("sps", s, g)][:, lo:hi],
-                    scalar1=t_hi if direct else 1.0,
-                    scalar2=None,
-                    op0=ALU.subtract if direct else ALU.mult,
-                    op1=ALU.max,
-                    accum_out=st[("mx", s)][:, j : j + 1],
+            st[("z", s)] = clp.tile([P, N], F32, name="z", tag="z")
+            st[("d", s)] = work.tile([P, N], F32, name="d", tag="d")
+            st[("mx", s)] = small.tile([P, 4], F32, name="mx", tag="mx")
+            st[("nmx", s)] = 0
+            for i, (k0, k1) in enumerate(bank_runs(NRB - r)):
+                exit_max(
+                    s, st[("d", s)][:, (r + k0) * P : (r + k1) * P],
+                    st[("sps", s, i)][:, : (k1 - k0) * P], ALU.subtract, t_hi,
+                )
+
+        def exit_mirror(s):
+            for k0, k1 in bank_runs(s % NRB):
+                exit_max(
+                    s, st[("z", s)][:, k0 * P : k1 * P],
+                    st[("spm", s, k0)][:, : (k1 - k0) * P], ALU.mult, 1.0,
                 )
 
         def steep_mask(s):
@@ -131,20 +140,24 @@ def tile_sapmodule_t_kernel(tc, x, threshold, out):
                 out=st[("z", s)][:, r * P :], in0=d, scalar=STEEP, in1=d, op0=ALU.mult, op1=ALU.min
             )
 
-        def row_scalars(s):
+        def row_max(s):
             mx = st[("mx", s)]
-            last = len(st[("parts", s)]) - 1
+            last = st[("nmx", s)] - 1
             m = small.tile([P, 1], F32, name="m", tag="m")
-            nc.gpsimd.tensor_scalar(
+            nc.vector.tensor_scalar(
                 out=m[:], in0=mx[:, 0:1], scalar1=mx[:, 1:2], scalar2=mx[:, last : last + 1],
                 op0=ALU.max, op1=ALU.max,
             )
+            st[("m", s)] = m
+
+        def row_scalars(s):
+            m = st[("m", s)]
             negm = small.tile([P, 1], F32, name="negm", tag="negm")
-            nc.gpsimd.tensor_scalar(
+            nc.vector.tensor_scalar(
                 out=negm[:], in0=m[:], scalar1=0.0, scalar2=-scale, op0=ALU.max, op1=ALU.mult
             )
             rsc = small.tile([P, 1], F32, name="rsc", tag="rsc")
-            nc.gpsimd.tensor_scalar(
+            nc.vector.tensor_scalar(
                 out=rsc[:], in0=m[:], scalar1=0.0, scalar2=scale, op0=ALU.is_ge, op1=ALU.mult
             )
             st[("negm", s)] = negm
@@ -243,66 +256,83 @@ def tile_sapmodule_t_kernel(tc, x, threshold, out):
                 )
             st[("acc", h, cc)] = acc
 
-        def normalise(h, cc):
+        def drain_acc(h, cc):
             if cc == 0:
                 st[("osb", h)] = work.tile([P, NCC, HALF], F32, name="osb", tag="osb")
+            nc.scalar.copy(out=st[("osb", h)][:, cc, :], in_=st[("acc", h, cc)][:])
+
+        def scale_gpsimd(h, cc):
             dst = st[("osb", h)][:, cc, :]
-            src = st[("acc", h, cc)][:]
-            if cc in SG_BLOCKS and h < 2 * B - 1:
-                nc.scalar.copy(out=dst, in_=src)
-                nc.gpsimd.tensor_tensor(out=dst, in0=dst, in1=st[("rsb", h)][:], op=ALU.mult)
-            else:
-                nc.vector.tensor_tensor(out=dst, in0=src, in1=st[("rsb", h)][:], op=ALU.mult)
+            nc.gpsimd.tensor_tensor(out=dst, in0=dst, in1=st[("rsb", h)][:], op=ALU.mult)
+            store(h, cc)
+
+        def scale_vector(h, cc):
+            if cc == 0:
+                st[("osb", h)] = work.tile([P, NCC, HALF], F32, name="osb", tag="osb")
+            nc.vector.tensor_tensor(
+                out=st[("osb", h)][:, cc, :], in0=st[("acc", h, cc)][:], in1=st[("rsb", h)][:], op=ALU.mult
+            )
+            store(h, cc)
+
+        def store(h, cc):
             b, hh = divmod(h, 2)
+            st[("left", h)] = st.get(("left", h), NCC) - 1
             if h == 2 * B - 1:
                 nc.sync.dma_start(out=ov[b][:, cc, hh * HALF : (hh + 1) * HALF], in_=st[("osb", h)][:, cc, :])
-            elif cc == NCC - 1:
+            elif st[("left", h)] == 0:
                 nc.sync.dma_start(out=ov[b][:, :, hh * HALF : (hh + 1) * HALF], in_=st[("osb", h)][:])
 
         NS = B * NRB
         NH = 2 * B
         ctx.enter_context(tc.manual_schedule())
-        for t in range(-1, NS + 2):
+        def at(t, lag):
+            return divmod(t - lag, 4) if 0 <= t - lag < NS else (-1, -1)
+
+        for t in range(-1, NS + 12):
+            h, cc = at(t, 10)
+            if h >= 0 and cc in SG_BLOCKS:
+                scale_gpsimd(h, cc)
             if 0 <= t < NS:
-                s_mirror(t, 0)
-                s_mirror(t, 1)
+                s_mirror(t)
             if 0 <= t - 2 < NS:
                 e_transposes(t - 2)
+            if 0 <= t - 1 < NS:
+                exp_row(t - 1)
+            if 0 <= t - 2 < NS:
                 e_regroup(t - 2)
             if 0 <= t < NS and t % NRB in (0, 2, 3, 4):
                 k = (0, 2, 3, 4).index(t % NRB)
                 f_transposes(t // NRB, k // 2, k % 2)
-            if t >= 5 and (t - 5) % 4 == 0 and (t - 5) // 4 < NH:
-                rs_broadcast((t - 5) // 4)
+            h, cc = at(t, 6)
+            if cc == 0:
+                rs_broadcast(h)
             if 0 <= t < NS:
-                exit_max(t, 0)
-                exit_max(t, 1)
-                row_scalars(t)
+                exit_direct(t)
+                exit_mirror(t)
                 steep_mask(t)
-            if t >= 8 and (t - 8) // 4 < NH and (t - 8) % 4 in SG_BLOCKS:
-                normalise((t - 8) // 4, (t - 8) % 4)
-            if 0 <= t < NS:
-                exp_row(t)
+                row_max(t)
+            h, cc = at(t, 9)
+            if h >= 0 and cc in SG_BLOCKS:
+                drain_acc(h, cc)
             if 0 <= t + 1 < NS:
                 s_matmuls(t + 1, 0)
-            if t >= 7 and (t - 7) // 4 < NH:
-                mx_block((t - 7) // 4, (t - 7) % 4)
+            h, cc = at(t, 8)
+            if h >= 0:
+                mx_block(h, cc)
             if 0 <= t + 1 < NS:
                 s_matmuls(t + 1, 1)
-            if t >= 8 and (t - 8) // 4 < NH and (t - 8) % 4 not in SG_BLOCKS:
-                normalise((t - 8) // 4, (t - 8) % 4)
-            if 0 <= t - 1 < NS and (t - 1) % 4 == 3:
-                rs_recip((t - 1) // 4)
-            if 0 <= t < NS and t % NRB == 4:
-                f_quant(t // NRB)
-            if t >= 5 and (t - 5) % 4 == 0 and (t - 5) // 4 < NH - 1:
-                e_quant((t - 5) // 4)
-        mx_block(NH - 2, 3)
-        normalise(NH - 2, 2)
-        normalise(NH - 2, 3)
-        e_quant(NH - 1)
-        mx_block(NH - 1, 0)
-        for cc in range(1, NCC):
-            mx_block(NH - 1, cc)
-            normalise(NH - 1, cc - 1)
-        normalise(NH - 1, NCC - 1)
+            h, cc = at(t, 9)
+            if h >= 0 and cc not in SG_BLOCKS:
+                scale_vector(h, cc)
+            h, cc = at(t - 3, 2)
+            if cc == 0:
+                rs_recip(h)
+            if t % NRB == 5%NRB and 0 <= t - 5 < NS:
+                f_quant((t - 5) // NRB)
+            if 0 <= t < NS and 0:
+                row_scalars(t)
+            h, cc = at(t, 6)
+            if cc == 0:
+                e_quant(h)
+            if 0 <= t < NS and not 0:
+                row_scalars(t)

@@ -20,8 +20,9 @@ NCC = C // P
 NRB = N // P
 HALF = 512
 FLOPS = 2 * 2 * B * N * N * C
-SG_BLOCKS = (0, 1, 3)
+SG_BLOCKS = (0, 1, 2, 3)
 STEEP = 2.0 ** 40
+WARM = 5
 
 
 def threshold_pair(t):
@@ -50,8 +51,8 @@ def tile_sapmodule_t_kernel(tc, x, threshold, out):
         const = ctx.enter_context(tc.tile_pool(name="const", bufs=1))
         xpool = ctx.enter_context(tc.tile_pool(name="xpool", bufs=1))
         work = ctx.enter_context(tc.tile_pool(name="work", bufs=3))
-        clp = ctx.enter_context(tc.tile_pool(name="clp", bufs=11))
-        small = ctx.enter_context(tc.tile_pool(name="small", bufs=4))
+        clp = ctx.enter_context(tc.tile_pool(name="clp", bufs=16))
+        small = ctx.enter_context(tc.tile_pool(name="small", bufs=8))
         mxp = ctx.enter_context(tc.tile_pool(name="mxp", bufs=2))
         ps_s = ctx.enter_context(tc.psum_pool(name="ps_s", bufs=4))
         ps_t = ctx.enter_context(tc.psum_pool(name="ps_t", bufs=2))
@@ -73,6 +74,12 @@ def tile_sapmodule_t_kernel(tc, x, threshold, out):
         make_identity(nc, ident_f[:])
 
         st = {}
+
+        warm = const.tile([P, HALF], BF16, name="warm")
+        nc.vector.memset(warm[:], 0.0)
+        wps = ps_o.tile([P, HALF], F32, name="wps", tag="acc")
+        for i in range(WARM):
+            nc.tensor.matmul(out=wps[:], lhsT=warm[:, :P], rhs=warm[:], start=True, stop=True)
 
         def bank_runs(n_blocks):
             return [(k, min(k + 4, n_blocks)) for k in range(0, n_blocks, 4)]
@@ -106,31 +113,40 @@ def tile_sapmodule_t_kernel(tc, x, threshold, out):
                         ident_f[:],
                     )
 
-        def exit_max(s, out, in_, op0, scalar1):
-            j = st[("nmx", s)]
-            st[("nmx", s)] = j + 1
+        def exit_max(out, in_, op0, scalar1, init, accum):
             nc.vector.tensor_scalar(
-                out=out, in0=in_, scalar1=scalar1, scalar2=None, op0=op0, op1=ALU.max,
-                accum_out=st[("mx", s)][:, j : j + 1],
+                out=out, in0=in_, scalar1=scalar1, scalar2=init, op0=op0, op1=ALU.max, accum_out=accum
             )
 
         def exit_direct(s):
             r = s % NRB
             st[("z", s)] = clp.tile([P, N], F32, name="z", tag="z")
             st[("d", s)] = work.tile([P, N], F32, name="d", tag="d")
-            st[("mx", s)] = small.tile([P, 4], F32, name="mx", tag="mx")
-            st[("nmx", s)] = 0
-            for i, (k0, k1) in enumerate(bank_runs(NRB - r)):
+            if s % 2 == 0:
+                st[("mx", s // 2)] = small.tile([P, 3, 2], F32, name="mx", tag="mx")
+            mx = st[("mx", s // 2)]
+            runs = bank_runs(NRB - r)
+            for i, (k0, k1) in enumerate(runs):
                 exit_max(
-                    s, st[("d", s)][:, (r + k0) * P : (r + k1) * P],
-                    st[("sps", s, i)][:, : (k1 - k0) * P], ALU.subtract, t_hi,
+                    st[("d", s)][:, (r + k0) * P : (r + k1) * P], st[("sps", s, i)][:, : (k1 - k0) * P],
+                    ALU.subtract, t_hi, None, mx[:, direct_slot(r, i), s % 2 : s % 2 + 1],
                 )
 
+        def direct_slot(r, i):
+            if r == 0 or r == 4:
+                return i
+            return 2 if i == 0 else 0
+
         def exit_mirror(s):
-            for k0, k1 in bank_runs(s % NRB):
+            r = s % NRB
+            mx = st[("mx", s // 2)]
+            runs = bank_runs(r)
+            for i, (k0, k1) in enumerate(runs):
+                takes_up = r != 4 and i == len(runs) - 1
                 exit_max(
-                    s, st[("z", s)][:, k0 * P : k1 * P],
-                    st[("spm", s, k0)][:, : (k1 - k0) * P], ALU.mult, 1.0,
+                    st[("z", s)][:, k0 * P : k1 * P], st[("spm", s, k0)][:, : (k1 - k0) * P],
+                    ALU.mult, 1.0, mx[:, 2, s % 2 : s % 2 + 1] if takes_up else None,
+                    mx[:, 0 if (r > 4 and i == 0) else 1, s % 2 : s % 2 + 1],
                 )
 
         def steep_mask(s):
@@ -140,28 +156,24 @@ def tile_sapmodule_t_kernel(tc, x, threshold, out):
                 out=st[("z", s)][:, r * P :], in0=d, scalar=STEEP, in1=d, op0=ALU.mult, op1=ALU.min
             )
 
-        def row_max(s):
-            mx = st[("mx", s)]
-            last = st[("nmx", s)] - 1
-            m = small.tile([P, 1], F32, name="m", tag="m")
-            nc.vector.tensor_scalar(
-                out=m[:], in0=mx[:, 0:1], scalar1=mx[:, 1:2], scalar2=mx[:, last : last + 1],
-                op0=ALU.max, op1=ALU.max,
-            )
-            st[("m", s)] = m
+        def pair_max(j):
+            m = small.tile([P, 2], F32, name="m", tag="m")
+            mx = st[("mx", j)]
+            nc.vector.tensor_tensor(out=m[:], in0=mx[:, 0, :], in1=mx[:, 1, :], op=ALU.max)
+            st[("m", j)] = m
 
-        def row_scalars(s):
-            m = st[("m", s)]
-            negm = small.tile([P, 1], F32, name="negm", tag="negm")
+        def pair_scalars(j):
+            m = st[("m", j)]
+            negm = small.tile([P, 2], F32, name="negm", tag="negm")
             nc.vector.tensor_scalar(
                 out=negm[:], in0=m[:], scalar1=0.0, scalar2=-scale, op0=ALU.max, op1=ALU.mult
             )
-            rsc = small.tile([P, 1], F32, name="rsc", tag="rsc")
+            rsc = small.tile([P, 2], F32, name="rsc", tag="rsc")
             nc.vector.tensor_scalar(
                 out=rsc[:], in0=m[:], scalar1=0.0, scalar2=scale, op0=ALU.is_ge, op1=ALU.mult
             )
-            st[("negm", s)] = negm
-            st[("rsc", s)] = rsc
+            st[("negm", j)] = negm
+            st[("rsc", j)] = rsc
 
         def exp_row(s):
             h, rl = divmod(s, 4)
@@ -170,7 +182,7 @@ def tile_sapmodule_t_kernel(tc, x, threshold, out):
             ebf = work.tile([P, N], BF16, name="ebf", tag="ebf", bufs=4)
             nc.scalar.activation(
                 out=ebf[:], in_=st[("z", s)][:], func=ACT.Exp,
-                bias=st[("negm", s)][:, 0:1], scale=st[("rsc", s)][:, 0:1],
+                bias=st[("negm", s // 2)][:, s % 2 : s % 2 + 1], scale=st[("rsc", s // 2)][:, s % 2 : s % 2 + 1],
                 accum_out=st[("ssum", h)][:, rl : rl + 1],
             )
             st[("ebf", s)] = ebf
@@ -192,38 +204,43 @@ def tile_sapmodule_t_kernel(tc, x, threshold, out):
                 in_=st[("tp", s)][:].rearrange("p (g u) i -> p g i u", g=2),
             )
 
-        def e_quant(h):
-            ecod = mxp.tile([P, 2 * HALF], U32, name="ecod", tag="ecod", align_bytes=64)
-            esc = mxp.tile([P, 2 * HALF], U8, name="esc", tag="esc", align_bytes=64)
+        def e_quant(h, g):
+            if g == 0:
+                st[("ecod", h)] = mxp.tile([P, 2 * HALF], U32, name="ecod", tag="ecod", align_bytes=64)
+                st[("esc", h)] = mxp.tile([P, 2 * HALF], U8, name="esc", tag="esc", align_bytes=64)
+            cols = slice(g * HALF, (g + 1) * HALF)
             nc.vector.quantize_mx(
-                out=ecod[:].bitcast(FP8X4), scales=esc[:],
-                in_=st[("grp", h)][:],
+                out=st[("ecod", h)][:, cols].bitcast(FP8X4), scales=st[("esc", h)][:, cols],
+                in_=st[("grp", h)][:, g * 4 * HALF : (g + 1) * 4 * HALF],
             )
-            st[("ecod", h)] = ecod
-            st[("esc", h)] = esc
 
         def f_transposes(b, g, cp):
             xw = xs[b][:].rearrange("p cc n -> p (cc n)").bitcast(F32)
             ft = ps_t.tile([P, 2, 2 * P], F32, name="ft", tag="tp")
             for u in range(2):
                 for c2 in range(2):
-                    cc = 2 * cp + c2
-                    w0 = cc * (N // 2) + (2 * g + u) * P
+                    w0 = (2 * cp + c2) * (N // 2) + (2 * g + u) * P
                     nc.tensor.transpose(ft[:, u, c2 * P : (c2 + 1) * P], xw[:, w0 : w0 + P], ident_f[:])
+            st[("ft", b, g, cp)] = ft
+
+        def f_regroup(b, g, cp):
             if g == 0 and cp == 0:
                 st[("fgrp", b)] = mxp.tile([P, 4 * N], BF16, name="fgrp", tag="fgrp", align_bytes=64)
             fgw = st[("fgrp", b)][:].bitcast(F32).rearrange("p (g c u) -> p g c u", g=2, u=2)
             nc.scalar.copy(
                 out=fgw[:, g, cp * 2 * P : (cp + 1) * 2 * P, :],
-                in_=ft[:].rearrange("p u c -> p c u"),
+                in_=st[("ft", b, g, cp)][:].rearrange("p u c -> p c u"),
             )
 
-        def f_quant(b):
-            fcod = mxp.tile([P, 2 * C], U32, name="fcod", tag="fcod", align_bytes=64)
-            fsc = mxp.tile([P, 2 * C], U8, name="fsc", tag="fsc", align_bytes=64)
-            nc.vector.quantize_mx(out=fcod[:].bitcast(FP8X4), scales=fsc[:], in_=st[("fgrp", b)][:])
-            st[("fcod", b)] = fcod
-            st[("fsc", b)] = fsc
+        def f_quant(b, g):
+            if g == 0:
+                st[("fcod", b)] = mxp.tile([P, 2 * C], U32, name="fcod", tag="fcod", align_bytes=64)
+                st[("fsc", b)] = mxp.tile([P, 2 * C], U8, name="fsc", tag="fsc", align_bytes=64)
+            cols = slice(g * C, (g + 1) * C)
+            nc.vector.quantize_mx(
+                out=st[("fcod", b)][:, cols].bitcast(FP8X4), scales=st[("fsc", b)][:, cols],
+                in_=st[("fgrp", b)][:, g * 4 * C : (g + 1) * 4 * C],
+            )
 
         def rs_recip(h):
             rsv = small.tile([P, 4], F32, name="rsv", tag="rsv")
@@ -237,8 +254,11 @@ def tile_sapmodule_t_kernel(tc, x, threshold, out):
                 nc.tensor.transpose(
                     bc[:, rl * P : (rl + 1) * P], rsv[:, rl : rl + 1].to_broadcast([P, P]), ident_f[:]
                 )
+            st[("bc", h)] = bc
+
+        def rs_copy(h):
             rsb = mxp.tile([P, HALF], F32, name="rsb", tag="rsb")
-            nc.scalar.copy(out=rsb[:], in_=bc[:])
+            nc.scalar.copy(out=rsb[:], in_=st[("bc", h)][:])
             st[("rsb", h)] = rsb
 
         def mx_block(h, cc):
@@ -277,62 +297,142 @@ def tile_sapmodule_t_kernel(tc, x, threshold, out):
         def store(h, cc):
             b, hh = divmod(h, 2)
             st[("left", h)] = st.get(("left", h), NCC) - 1
-            if h == 2 * B - 1:
-                nc.sync.dma_start(out=ov[b][:, cc, hh * HALF : (hh + 1) * HALF], in_=st[("osb", h)][:, cc, :])
-            elif st[("left", h)] == 0:
+            if st[("left", h)] == 0:
                 nc.sync.dma_start(out=ov[b][:, :, hh * HALF : (hh + 1) * HALF], in_=st[("osb", h)][:])
+
+        def last_quant(s):
+            h, rl = divmod(s, 4)
+            if rl == 0:
+                st[("ecod", h)] = mxp.tile([P, 2 * HALF], U32, name="ecod", tag="ecod", align_bytes=64)
+                st[("esc", h)] = mxp.tile([P, 2 * HALF], U8, name="esc", tag="esc", align_bytes=64)
+            for g in range(2):
+                c0 = g * HALF + rl * P
+                nc.vector.quantize_mx(
+                    out=st[("ecod", h)][:, c0 : c0 + P].bitcast(FP8X4), scales=st[("esc", h)][:, c0 : c0 + P],
+                    in_=st[("grp", h)][:, 4 * c0 : 4 * (c0 + P)],
+                )
+
+        def last_recip(s):
+            h, rl = divmod(s, 4)
+            if rl == 0:
+                st[("rsv", h)] = small.tile([P, 4], F32, name="rsv", tag="rsv")
+            nc.vector.reciprocal(out=st[("rsv", h)][:, rl : rl + 1], in_=st[("ssum", h)][:, rl : rl + 1])
+
+        def last_broadcast(s):
+            h, rl = divmod(s, 4)
+            bc = ps_t.tile([P, HALF], F32, name="lbc", tag="tp")
+            nc.tensor.transpose(bc[:, :P], st[("rsv", h)][:, rl : rl + 1].to_broadcast([P, P]), ident_f[:])
+            st[("bc", s)] = bc
+
+        def last_rs_copy(s):
+            rsb = small.tile([P, P], F32, name="lrsb", tag="lrsb")
+            nc.scalar.copy(out=rsb[:], in_=st[("bc", s)][:, :P])
+            st[("lrsb", s)] = rsb
+
+        def last_mx(s):
+            h, rl = divmod(s, 4)
+            b = h // 2
+            acc = ps_s.tile([P, NCC, P], F32, name="lacc", tag="sps")
+            for cc in range(NCC):
+                for g in range(2):
+                    f0 = g * C + cc * P
+                    c0 = g * HALF + rl * P
+                    nc.tensor.matmul_mx(
+                        out=acc[:, cc, :],
+                        lhsT=st[("fcod", b)][:, f0 : f0 + P].bitcast(FP8X4),
+                        lhsT_scale=st[("fsc", b)][:, f0 : f0 + P],
+                        rhs=st[("ecod", h)][:, c0 : c0 + P].bitcast(FP8X4),
+                        rhs_scale=st[("esc", h)][:, c0 : c0 + P],
+                        start=(g == 0),
+                        stop=(g == 1),
+                    )
+            st[("lacc", s)] = acc
+
+        def last_scale(s):
+            b, r = divmod(s, NRB)
+            osr = work.tile([P, NCC, P], F32, name="osr", tag="osr")
+            nc.vector.tensor_tensor(
+                out=osr[:], in0=st[("lacc", s)][:],
+                in1=st[("lrsb", s)][:].unsqueeze(1).to_broadcast([P, NCC, P]), op=ALU.mult,
+            )
+            nc.sync.dma_start(out=ov[b][:, :, r * P : (r + 1) * P], in_=osr[:])
 
         NS = B * NRB
         NH = 2 * B
         ctx.enter_context(tc.manual_schedule())
-        def at(t, lag):
-            return divmod(t - lag, 4) if 0 <= t - lag < NS else (-1, -1)
 
-        for t in range(-1, NS + 12):
-            h, cc = at(t, 10)
+        def at(t, lag):
+            return divmod(t - lag, 4) if 0 <= t - lag < NS - 4 else (-1, -1)
+
+        for t in range(-2, NS + 13):
+            h, cc = at(t, 12)
             if h >= 0 and cc in SG_BLOCKS:
                 scale_gpsimd(h, cc)
-            if 0 <= t < NS:
-                s_mirror(t)
-            if 0 <= t - 2 < NS:
-                e_transposes(t - 2)
-            if 0 <= t - 1 < NS:
-                exp_row(t - 1)
-            if 0 <= t - 2 < NS:
-                e_regroup(t - 2)
-            if 0 <= t < NS and t % NRB in (0, 2, 3, 4):
-                k = (0, 2, 3, 4).index(t % NRB)
-                f_transposes(t // NRB, k // 2, k % 2)
-            h, cc = at(t, 6)
+            if 0 <= t - 0 < NS:
+                s_mirror(t - 0)
+            h, cc = at(t, 7)
             if cc == 0:
                 rs_broadcast(h)
-            if 0 <= t < NS:
-                exit_direct(t)
-                exit_mirror(t)
-                steep_mask(t)
-                row_max(t)
-            h, cc = at(t, 9)
-            if h >= 0 and cc in SG_BLOCKS:
-                drain_acc(h, cc)
-            if 0 <= t + 1 < NS:
-                s_matmuls(t + 1, 0)
+            if 0 <= t - 3 < NS:
+                e_transposes(t - 3)
+            if 0 <= t - 0 < NS and (t - 0) % 2 == 0:
+                b, k = divmod((t - 0) // 2, 4)
+                f_transposes(b, k // 2, k % 2)
             h, cc = at(t, 8)
             if h >= 0:
                 mx_block(h, cc)
-            if 0 <= t + 1 < NS:
-                s_matmuls(t + 1, 1)
-            h, cc = at(t, 9)
-            if h >= 0 and cc not in SG_BLOCKS:
-                scale_vector(h, cc)
-            h, cc = at(t - 3, 2)
+            if NS - 4 <= t - 4 < NS:
+                last_broadcast(t - 4)
+            if 0 <= t - 2 < NS:
+                exp_row(t - 2)
+            if 0 <= t - 3 < NS:
+                e_regroup(t - 3)
+            if 0 <= t - 0 < NS and (t - 0) % 2 == 0:
+                b, k = divmod((t - 0) // 2, 4)
+                f_regroup(b, k // 2, k % 2)
+            h, cc = at(t, 7)
             if cc == 0:
-                rs_recip(h)
-            if t % NRB == 5%NRB and 0 <= t - 5 < NS:
-                f_quant((t - 5) // NRB)
-            if 0 <= t < NS and 0:
-                row_scalars(t)
+                rs_copy(h)
+            if NS - 4 <= t - 4 < NS:
+                last_rs_copy(t - 4)
+            h, cc = at(t, 8)
+            if h >= 0 and cc in SG_BLOCKS:
+                drain_acc(h, cc)
+            if 0 <= t - 0 < NS:
+                exit_direct(t - 0)
+            if 0 <= t - 0 < NS:
+                exit_mirror(t - 0)
+            if NS - 4 <= t - 3 < NS:
+                last_recip(t - 3)
+            if 0 <= t - 0 < NS and (t - 0) % 2 == 1:
+                pair_max((t - 0) // 2)
+            if 0 <= t - 0 < NS:
+                steep_mask(t - 0)
             h, cc = at(t, 6)
             if cc == 0:
-                e_quant(h)
-            if 0 <= t < NS and not 0:
-                row_scalars(t)
+                rs_recip(h)
+            if 0 <= t - 4 < NS and (t - 4) % 8 == 0:
+                f_quant((t - 4) // 8, 0)
+            if 0 <= t - 7 < NS and (t - 7) % 8 == 0:
+                f_quant((t - 7) // 8, 1)
+            h, cc = at(t, 6)
+            if cc == 0:
+                e_quant(h, 0)
+            h, cc = at(t, 7)
+            if cc == 0:
+                e_quant(h, 1)
+            if 0 <= t - 0 < NS and (t - 0) % 2 == 1:
+                pair_scalars((t - 0) // 2)
+            if NS - 4 <= t - 6 < NS:
+                last_scale(t - 6)
+            if NS - 4 <= t - 4 < NS:
+                last_quant(t - 4)
+            if NS - 4 <= t - 4 < NS:
+                last_mx(t - 4)
+            if 0 <= t + 1 < NS:
+                s_matmuls(t + 1, 0)
+            if 0 <= t + 1 < NS:
+                s_matmuls(t + 1, 1)
+            h, cc = at(t, 12)
+            if h >= 0 and cc not in SG_BLOCKS:
+                scale_vector(h, cc)

@@ -365,8 +365,10 @@ def tile_sapmodule_t_kernel(tc, x, threshold, out):
             return divmod(t - lag, 4) if 0 <= t - lag < NS - 4 else (-1, -1)
 
         for t in range(-2, NS + 13):
+            if NS - 4 <= t - 6 < NS:
+                last_scale(t - 6)
             h, cc = at(t, 12)
-            if h >= 0 and cc in SG_BLOCKS:
+            if h >= 0 and (h < 5):
                 scale_gpsimd(h, cc)
             if 0 <= t - 0 < NS:
                 s_mirror(t - 0)
@@ -396,7 +398,7 @@ def tile_sapmodule_t_kernel(tc, x, threshold, out):
             if NS - 4 <= t - 4 < NS:
                 last_rs_copy(t - 4)
             h, cc = at(t, 8)
-            if h >= 0 and cc in SG_BLOCKS:
+            if h >= 0 and (h < 5):
                 drain_acc(h, cc)
             if 0 <= t - 0 < NS:
                 exit_direct(t - 0)
@@ -408,6 +410,11 @@ def tile_sapmodule_t_kernel(tc, x, threshold, out):
                 pair_max((t - 0) // 2)
             if 0 <= t - 0 < NS:
                 steep_mask(t - 0)
+            if 0 <= t - 0 < NS and (t - 0) % 2 == 1:
+                pair_scalars((t - 0) // 2)
+            h, cc = at(t, 9)
+            if h >= 0 and not (h < 5):
+                scale_vector(h, cc)
             h, cc = at(t, 6)
             if cc == 0:
                 rs_recip(h)
@@ -418,13 +425,9 @@ def tile_sapmodule_t_kernel(tc, x, threshold, out):
             h, cc = at(t, 6)
             if cc == 0:
                 e_quant(h, 0)
-            h, cc = at(t, 7)
+            h, cc = at(t, 6)
             if cc == 0:
                 e_quant(h, 1)
-            if 0 <= t - 0 < NS and (t - 0) % 2 == 1:
-                pair_scalars((t - 0) // 2)
-            if NS - 4 <= t - 6 < NS:
-                last_scale(t - 6)
             if NS - 4 <= t - 4 < NS:
                 last_quant(t - 4)
             if NS - 4 <= t - 4 < NS:
@@ -433,6 +436,3 @@ def tile_sapmodule_t_kernel(tc, x, threshold, out):
                 s_matmuls(t + 1, 0)
             if 0 <= t + 1 < NS:
                 s_matmuls(t + 1, 1)
-            h, cc = at(t, 12)
-            if h >= 0 and cc not in SG_BLOCKS:
-                scale_vector(h, cc)

@@ -84,17 +84,17 @@ def tile_sapmodule_t_kernel(tc, x, threshold, out):
         def bank_runs(n_blocks):
             return [(k, min(k + 4, n_blocks)) for k in range(0, n_blocks, 4)]
 
-        def s_matmuls(s, i):
+        def s_matmuls(s, i, half):
             b, r = divmod(s, NRB)
             runs = bank_runs(NRB - r)
             if i >= len(runs):
                 return
             k0, k1 = runs[i]
-            sps = ps_s.tile([P, HALF], F32, name="sps", tag="sps")
-            st[("sps", s, i)] = sps
-            for cc in range(NCC):
+            if half == 0:
+                st[("sps", s, i)] = ps_s.tile([P, HALF], F32, name="sps", tag="sps")
+            for cc in (2 * half, 2 * half + 1):
                 nc.tensor.matmul(
-                    out=sps[:, : (k1 - k0) * P],
+                    out=st[("sps", s, i)][:, : (k1 - k0) * P],
                     lhsT=xs[b][:, cc, r * P : (r + 1) * P],
                     rhs=xs[b][:, cc, (r + k0) * P : (r + k1) * P],
                     start=(cc == 0),
@@ -364,75 +364,79 @@ def tile_sapmodule_t_kernel(tc, x, threshold, out):
         def at(t, lag):
             return divmod(t - lag, 4) if 0 <= t - lag < NS - 4 else (-1, -1)
 
-        for t in range(-2, NS + 13):
-            if NS - 4 <= t - 6 < NS:
-                last_scale(t - 6)
-            h, cc = at(t, 12)
-            if h >= 0 and (h < 5):
-                scale_gpsimd(h, cc)
-            if 0 <= t - 0 < NS:
-                s_mirror(t - 0)
-            h, cc = at(t, 7)
-            if cc == 0:
-                rs_broadcast(h)
-            if 0 <= t - 3 < NS:
-                e_transposes(t - 3)
-            if 0 <= t - 0 < NS and (t - 0) % 2 == 0:
-                b, k = divmod((t - 0) // 2, 4)
-                f_transposes(b, k // 2, k % 2)
-            h, cc = at(t, 8)
-            if h >= 0:
-                mx_block(h, cc)
-            if NS - 4 <= t - 4 < NS:
-                last_broadcast(t - 4)
+        for t in range(-2, NS + 10):
+            if NS - 4 <= t - 7 < NS:
+                last_scale(t - 7)
             if 0 <= t - 2 < NS:
                 exp_row(t - 2)
-            if 0 <= t - 3 < NS:
-                e_regroup(t - 3)
-            if 0 <= t - 0 < NS and (t - 0) % 2 == 0:
-                b, k = divmod((t - 0) // 2, 4)
+            if 0 <= t - 1 < NS and (t - 1) % 2 == 0:
+                b, k = divmod((t - 1) // 2, 4)
                 f_regroup(b, k // 2, k % 2)
-            h, cc = at(t, 7)
-            if cc == 0:
-                rs_copy(h)
-            if NS - 4 <= t - 4 < NS:
-                last_rs_copy(t - 4)
-            h, cc = at(t, 8)
-            if h >= 0 and (h < 5):
-                drain_acc(h, cc)
             if 0 <= t - 0 < NS:
                 exit_direct(t - 0)
             if 0 <= t - 0 < NS:
+                s_mirror(t - 0)
+            if 0 <= t + 1 < NS:
+                s_matmuls(t + 1, 0, 0)
+            if 0 <= t - 3 < NS:
+                e_transposes(t - 3)
+            if NS - 4 <= t - 4 < NS:
+                last_broadcast(t - 4)
+            if 0 <= t + 1 < NS:
+                s_matmuls(t + 1, 0, 1)
+            if 0 <= t - 0 < NS and (t - 0) % 2 == 0:
+                b, k = divmod((t - 0) // 2, 4)
+                f_transposes(b, k // 2, k % 2)
+            if NS - 4 <= t - 5 < NS:
+                last_mx(t - 5)
+            if 0 <= t + 1 < NS:
+                s_matmuls(t + 1, 1, 0)
+            h, cc = at(t, 7)
+            if cc == 0:
+                rs_broadcast(h)
+            h, cc = at(t, 8)
+            if h >= 0:
+                mx_block(h, cc)
+            if 0 <= t + 1 < NS:
+                s_matmuls(t + 1, 1, 1)
+            if 0 <= t - 3 < NS:
+                e_regroup(t - 3)
+            h, cc = at(t, 9)
+            if h >= 0 and (h < 5 and cc != 2):
+                drain_acc(h, cc)
+            if NS - 4 <= t - 4 < NS:
+                last_rs_copy(t - 4)
+            h, cc = at(t, 7)
+            if cc == 0:
+                rs_copy(h)
+            if 0 <= t - 0 < NS:
                 exit_mirror(t - 0)
-            if NS - 4 <= t - 3 < NS:
-                last_recip(t - 3)
+            h, cc = at(t, 9)
+            if h >= 0 and not (h < 5 and cc != 2):
+                scale_vector(h, cc)
             if 0 <= t - 0 < NS and (t - 0) % 2 == 1:
                 pair_max((t - 0) // 2)
             if 0 <= t - 0 < NS:
                 steep_mask(t - 0)
             if 0 <= t - 0 < NS and (t - 0) % 2 == 1:
                 pair_scalars((t - 0) // 2)
-            h, cc = at(t, 9)
-            if h >= 0 and not (h < 5):
-                scale_vector(h, cc)
             h, cc = at(t, 6)
             if cc == 0:
                 rs_recip(h)
-            if 0 <= t - 4 < NS and (t - 4) % 8 == 0:
-                f_quant((t - 4) // 8, 0)
-            if 0 <= t - 7 < NS and (t - 7) % 8 == 0:
-                f_quant((t - 7) // 8, 1)
-            h, cc = at(t, 6)
-            if cc == 0:
-                e_quant(h, 0)
-            h, cc = at(t, 6)
-            if cc == 0:
-                e_quant(h, 1)
+            if NS - 4 <= t - 3 < NS:
+                last_recip(t - 3)
             if NS - 4 <= t - 4 < NS:
                 last_quant(t - 4)
-            if NS - 4 <= t - 4 < NS:
-                last_mx(t - 4)
-            if 0 <= t + 1 < NS:
-                s_matmuls(t + 1, 0)
-            if 0 <= t + 1 < NS:
-                s_matmuls(t + 1, 1)
+            if 0 <= t - 5 < NS and (t - 5) % 8 == 0:
+                f_quant((t - 5) // 8, 0)
+            if 0 <= t - 7 < NS and (t - 7) % 8 == 0:
+                f_quant((t - 7) // 8, 1)
+            h, cc = at(t, 7)
+            if cc == 0:
+                e_quant(h, 0)
+            h, cc = at(t, 7)
+            if cc == 0:
+                e_quant(h, 1)
+            h, cc = at(t, 9)
+            if h >= 0 and (h < 5 and cc != 2):
+                scale_gpsimd(h, cc)

@@ -63,10 +63,8 @@ def tile_sapmodule_t_kernel(tc, x, threshold, out):
             xt = xpool.tile([P, NCC, N], BF16, name="x%d" % b)
             xs.append(xt)
             if b == 0:
-                for g in range(2):
-                    nc.sync.dma_start(
-                        out=xt[:, :, g * HALF : (g + 1) * HALF], in_=xv[b][:, :, g * HALF : (g + 1) * HALF]
-                    )
+                for cc in range(NCC):
+                    nc.sync.dma_start(out=xt[:, cc, :], in_=xv[b][:, cc, :])
             else:
                 nc.sync.dma_start(out=xt[:], in_=xv[b])
 
@@ -87,14 +85,16 @@ def tile_sapmodule_t_kernel(tc, x, threshold, out):
         def s_matmuls(s, i, half):
             b, r = divmod(s, NRB)
             runs = bank_runs(NRB - r)
-            if i >= len(runs):
-                return
-            k0, k1 = runs[i]
-            if half == 0:
-                st[("sps", s, i)] = ps_s.tile([P, HALF], F32, name="sps", tag="sps")
-            for cc in (2 * half, 2 * half + 1):
+            parts = [(j, cc) for j in range(len(runs)) for cc in range(NCC)]
+            if s == 0:
+                parts = [(j, cc) for cc in range(NCC) for j in range(len(runs))]
+            q = 2 * i + half
+            for j, cc in parts[2 * q : 2 * q + 2]:
+                k0, k1 = runs[j]
+                if cc == 0:
+                    st[("sps", s, j)] = ps_s.tile([P, HALF], F32, name="sps", tag="sps")
                 nc.tensor.matmul(
-                    out=st[("sps", s, i)][:, : (k1 - k0) * P],
+                    out=st[("sps", s, j)][:, : (k1 - k0) * P],
                     lhsT=xs[b][:, cc, r * P : (r + 1) * P],
                     rhs=xs[b][:, cc, (r + k0) * P : (r + k1) * P],
                     start=(cc == 0),
@@ -263,7 +263,10 @@ def tile_sapmodule_t_kernel(tc, x, threshold, out):
 
         def mx_block(h, cc):
             b = h // 2
-            acc = ps_o.tile([P, HALF], F32, name="acc", tag="acc")
+            if h == 2 * B - 2:
+                acc = ps_s.tile([P, HALF], F32, name="acc6", tag="sps")
+            else:
+                acc = ps_o.tile([P, HALF], F32, name="acc", tag="acc")
             for g in range(2):
                 nc.tensor.matmul_mx(
                     out=acc[:],
@@ -332,7 +335,7 @@ def tile_sapmodule_t_kernel(tc, x, threshold, out):
         def last_mx(s):
             h, rl = divmod(s, 4)
             b = h // 2
-            acc = ps_s.tile([P, NCC, P], F32, name="lacc", tag="sps")
+            acc = ps_o.tile([P, NCC, P], F32, name="lacc", tag="acc")
             for cc in range(NCC):
                 for g in range(2):
                     f0 = g * C + cc * P
@@ -364,11 +367,28 @@ def tile_sapmodule_t_kernel(tc, x, threshold, out):
         def at(t, lag):
             return divmod(t - lag, 4) if 0 <= t - lag < NS - 4 else (-1, -1)
 
+        def rows(t, lag):
+            s = t - lag
+            if s == NS - 2:
+                return [s, s + 1]
+            return [s] if 0 <= s < NS - 2 else []
+
+        def last_rows(t, lag):
+            return [s for s in rows(t, lag) if s >= NS - 4]
+
+        def blocks(t, lag):
+            h, cc = at(t, lag)
+            if h < 0:
+                return []
+            if h < NH - 2:
+                return [(h, cc)]
+            return [(h, 2 * cc), (h, 2 * cc + 1)] if cc < 2 else []
+
         for t in range(-2, NS + 10):
-            if NS - 4 <= t - 7 < NS:
-                last_scale(t - 7)
-            if 0 <= t - 2 < NS:
-                exp_row(t - 2)
+            for s in last_rows(t, 6):
+                last_scale(s)
+            for s in rows(t, 2):
+                exp_row(s)
             if 0 <= t - 1 < NS and (t - 1) % 2 == 0:
                 b, k = divmod((t - 1) // 2, 4)
                 f_regroup(b, k // 2, k % 2)
@@ -378,42 +398,41 @@ def tile_sapmodule_t_kernel(tc, x, threshold, out):
                 s_mirror(t - 0)
             if 0 <= t + 1 < NS:
                 s_matmuls(t + 1, 0, 0)
-            if 0 <= t - 3 < NS:
-                e_transposes(t - 3)
-            if NS - 4 <= t - 4 < NS:
-                last_broadcast(t - 4)
+            for s in rows(t, 3):
+                e_transposes(s)
             if 0 <= t + 1 < NS:
                 s_matmuls(t + 1, 0, 1)
             if 0 <= t - 0 < NS and (t - 0) % 2 == 0:
                 b, k = divmod((t - 0) // 2, 4)
                 f_transposes(b, k // 2, k % 2)
-            if NS - 4 <= t - 5 < NS:
-                last_mx(t - 5)
             if 0 <= t + 1 < NS:
                 s_matmuls(t + 1, 1, 0)
             h, cc = at(t, 7)
             if cc == 0:
                 rs_broadcast(h)
-            h, cc = at(t, 8)
-            if h >= 0:
+            for s in last_rows(t, 5):
+                last_mx(s)
+            for h, cc in blocks(t, 8):
                 mx_block(h, cc)
             if 0 <= t + 1 < NS:
                 s_matmuls(t + 1, 1, 1)
-            if 0 <= t - 3 < NS:
-                e_regroup(t - 3)
-            h, cc = at(t, 9)
-            if h >= 0 and (h < 5 and cc != 2):
-                drain_acc(h, cc)
-            if NS - 4 <= t - 4 < NS:
-                last_rs_copy(t - 4)
+            for s in rows(t, 3):
+                e_regroup(s)
+            for s in last_rows(t, 4):
+                last_broadcast(s)
+            for h, cc in blocks(t, 9):
+                if (h < 5 and cc != 2):
+                    drain_acc(h, cc)
+            for s in last_rows(t, 4):
+                last_rs_copy(s)
             h, cc = at(t, 7)
             if cc == 0:
                 rs_copy(h)
             if 0 <= t - 0 < NS:
                 exit_mirror(t - 0)
-            h, cc = at(t, 9)
-            if h >= 0 and not (h < 5 and cc != 2):
-                scale_vector(h, cc)
+            for h, cc in blocks(t, 9):
+                if not (h < 5 and cc != 2):
+                    scale_vector(h, cc)
             if 0 <= t - 0 < NS and (t - 0) % 2 == 1:
                 pair_max((t - 0) // 2)
             if 0 <= t - 0 < NS:
@@ -423,10 +442,10 @@ def tile_sapmodule_t_kernel(tc, x, threshold, out):
             h, cc = at(t, 6)
             if cc == 0:
                 rs_recip(h)
-            if NS - 4 <= t - 3 < NS:
-                last_recip(t - 3)
-            if NS - 4 <= t - 4 < NS:
-                last_quant(t - 4)
+            for s in last_rows(t, 3):
+                last_recip(s)
+            for s in last_rows(t, 4):
+                last_quant(s)
             if 0 <= t - 5 < NS and (t - 5) % 8 == 0:
                 f_quant((t - 5) // 8, 0)
             if 0 <= t - 7 < NS and (t - 7) % 8 == 0:
@@ -437,6 +456,6 @@ def tile_sapmodule_t_kernel(tc, x, threshold, out):
             h, cc = at(t, 7)
             if cc == 0:
                 e_quant(h, 1)
-            h, cc = at(t, 9)
-            if h >= 0 and (h < 5 and cc != 2):
-                scale_gpsimd(h, cc)
+            for h, cc in blocks(t, 9):
+                if (h < 5 and cc != 2):
+                    scale_gpsimd(h, cc)

@@ -63,8 +63,10 @@ def tile_sapmodule_t_kernel(tc, x, threshold, out):
             xt = xpool.tile([P, NCC, N], BF16, name="x%d" % b)
             xs.append(xt)
             if b == 0:
-                for cc in range(NCC):
-                    nc.sync.dma_start(out=xt[:, cc, :], in_=xv[b][:, cc, :])
+                for g in range(2):
+                    nc.sync.dma_start(
+                        out=xt[:, :, g * HALF : (g + 1) * HALF], in_=xv[b][:, :, g * HALF : (g + 1) * HALF]
+                    )
             else:
                 nc.sync.dma_start(out=xt[:], in_=xv[b])
 
@@ -85,16 +87,14 @@ def tile_sapmodule_t_kernel(tc, x, threshold, out):
         def s_matmuls(s, i, half):
             b, r = divmod(s, NRB)
             runs = bank_runs(NRB - r)
-            parts = [(j, cc) for j in range(len(runs)) for cc in range(NCC)]
-            if s == 0:
-                parts = [(j, cc) for cc in range(NCC) for j in range(len(runs))]
-            q = 2 * i + half
-            for j, cc in parts[2 * q : 2 * q + 2]:
-                k0, k1 = runs[j]
-                if cc == 0:
-                    st[("sps", s, j)] = ps_s.tile([P, HALF], F32, name="sps", tag="sps")
+            if i >= len(runs):
+                return
+            k0, k1 = runs[i]
+            if half == 0:
+                st[("sps", s, i)] = ps_s.tile([P, HALF], F32, name="sps", tag="sps")
+            for cc in (2 * half, 2 * half + 1):
                 nc.tensor.matmul(
-                    out=st[("sps", s, j)][:, : (k1 - k0) * P],
+                    out=st[("sps", s, i)][:, : (k1 - k0) * P],
                     lhsT=xs[b][:, cc, r * P : (r + 1) * P],
                     rhs=xs[b][:, cc, (r + k0) * P : (r + k1) * P],
                     start=(cc == 0),

import math
from contextlib import ExitStack

import concourse.mybir as mybir
from concourse.masks import make_identity

F32 = mybir.dt.float32
BF16 = mybir.dt.bfloat16
U32 = mybir.dt.uint32
U8 = mybir.dt.uint8
FP8X4 = mybir.dt.float8_e4m3fn_x4
ALU = mybir.AluOpType
ACT = mybir.ActivationFunctionType

P = 128
B = 4
C = 512
N = 1024
NCC = C // P
NRB = N // P
HALF = 512
FLOPS = 2 * 2 * B * N * N * C
SG_BLOCKS = (0, 1, 2, 3)
STEEP = 2.0 ** 40
WARM = 5


def threshold_pair(t):
    unit = 1.0
    while t / unit >= 16777216.0:
        unit = unit * 2.0
    while t / unit < 8388608.0:
        unit = unit / 2.0
    y = t / unit
    lo = int(y)
    if lo == y:
        lo = lo - 1
    return lo * unit, (lo + 1) * unit


def tile_sapmodule_t_kernel(tc, x, threshold, out):
    nc = tc.nc
    assert threshold > 0.0
    scale = 1.0 / math.sqrt(C)
    t_hi = threshold_pair(threshold * math.sqrt(C))[1]

    xv = x.rearrange("b (p cc) h w -> b p cc (h w)", cc=NCC)
    ov = out.rearrange("b (m cc) h w -> b m cc (h w)", cc=NCC)

    with ExitStack() as ctx:
        const = ctx.enter_context(tc.tile_pool(name="const", bufs=1))
        xpool = ctx.enter_context(tc.tile_pool(name="xpool", bufs=1))
        work = ctx.enter_context(tc.tile_pool(name="work", bufs=3))
        clp = ctx.enter_context(tc.tile_pool(name="clp", bufs=16))
        small = ctx.enter_context(tc.tile_pool(name="small", bufs=8))
        mxp = ctx.enter_context(tc.tile_pool(name="mxp", bufs=2))
        ps_s = ctx.enter_context(tc.psum_pool(name="ps_s", bufs=4))
        ps_t = ctx.enter_context(tc.psum_pool(name="ps_t", bufs=2))
        ps_o = ctx.enter_context(tc.psum_pool(name="ps_o", bufs=2))

        xs = []
        for b in range(B):
            xt = xpool.tile([P, NCC, N], BF16, name="x%d" % b)
            xs.append(xt)
            if b == 0:
                for g in range(2):
                    nc.sync.dma_start(
                        out=xt[:, :, g * HALF : (g + 1) * HALF], in_=xv[b][:, :, g * HALF : (g + 1) * HALF]
                    )
            else:
                nc.sync.dma_start(out=xt[:], in_=xv[b])

        ident_f = const.tile([P, P], F32, name="ident_f")
        make_identity(nc, ident_f[:])

        st = {}

        warm = const.tile([P, HALF], BF16, name="warm")
        nc.vector.memset(warm[:], 0.0)
        wps = ps_o.tile([P, HALF], F32, name="wps", tag="acc")
        for i in range(WARM):
            nc.tensor.matmul(out=wps[:], lhsT=warm[:, :P], rhs=warm[:], start=True, stop=True)

        def bank_runs(n_blocks):
            return [(k, min(k + 4, n_blocks)) for k in range(0, n_blocks, 4)]

        def s_matmuls(s, i, half):
            b, r = divmod(s, NRB)
            runs = bank_runs(NRB - r)
            if i >= len(runs):
                return
            k0, k1 = runs[i]
            if half == 0:
                st[("sps", s, i)] = ps_s.tile([P, HALF], F32, name="sps", tag="sps")
            for cc in (2 * half, 2 * half + 1):
                nc.tensor.matmul(
                    out=st[("sps", s, i)][:, : (k1 - k0) * P],
                    lhsT=xs[b][:, cc, r * P : (r + 1) * P],
                    rhs=xs[b][:, cc, (r + k0) * P : (r + k1) * P],
                    start=(cc == 0),
                    stop=(cc == NCC - 1),
                )

        def s_mirror(s):
            b, r = divmod(s, NRB)
            for k0, k1 in bank_runs(r):
                spm = ps_s.tile([P, HALF], F32, name="spm", tag="sps")
                st[("spm", s, k0)] = spm
                for k in range(k0, k1):
                    nc.tensor.transpose(
                        spm[:, (k - k0) * P : (k - k0 + 1) * P],
                        st[("z", b * NRB + k)][:, r * P : (r + 1) * P],
                        ident_f[:],
                    )

        def exit_max(out, in_, op0, scalar1, init, accum):
            nc.vector.tensor_scalar(
                out=out, in0=in_, scalar1=scalar1, scalar2=init, op0=op0, op1=ALU.max, accum_out=accum
            )

        def exit_direct(s):
            r = s % NRB
            st[("z", s)] = clp.tile([P, N], F32, name="z", tag="z")
            st[("d", s)] = work.tile([P, N], F32, name="d", tag="d")
            if s % 2 == 0:
                st[("mx", s // 2)] = small.tile([P, 3, 2], F32, name="mx", tag="mx")
            mx = st[("mx", s // 2)]
            runs = bank_runs(NRB - r)
            for i, (k0, k1) in enumerate(runs):
                exit_max(
                    st[("d", s)][:, (r + k0) * P : (r + k1) * P], st[("sps", s, i)][:, : (k1 - k0) * P],
                    ALU.subtract, t_hi, None, mx[:, direct_slot(r, i), s % 2 : s % 2 + 1],
                )

        def direct_slot(r, i):
            if r == 0 or r == 4:
                return i
            return 2 if i == 0 else 0

        def exit_mirror(s):
            r = s % NRB
            mx = st[("mx", s // 2)]
            runs = bank_runs(r)
            for i, (k0, k1) in enumerate(runs):
                takes_up = r != 4 and i == len(runs) - 1
                exit_max(
                    st[("z", s)][:, k0 * P : k1 * P], st[("spm", s, k0)][:, : (k1 - k0) * P],
                    ALU.mult, 1.0, mx[:, 2, s % 2 : s % 2 + 1] if takes_up else None,
                    mx[:, 0 if (r > 4 and i == 0) else 1, s % 2 : s % 2 + 1],
                )

        def steep_mask(s):
            r = s % NRB
            d = st[("d", s)][:, r * P :]
            nc.vector.scalar_tensor_tensor(
                out=st[("z", s)][:, r * P :], in0=d, scalar=STEEP, in1=d, op0=ALU.mult, op1=ALU.min
            )

        def pair_max(j):
            m = small.tile([P, 2], F32, name="m", tag="m")
            mx = st[("mx", j)]
            nc.vector.tensor_tensor(out=m[:], in0=mx[:, 0, :], in1=mx[:, 1, :], op=ALU.max)
            st[("m", j)] = m

        def pair_scalars(j):
            m = st[("m", j)]
            negm = small.tile([P, 2], F32, name="negm", tag="negm")
            nc.vector.tensor_scalar(
                out=negm[:], in0=m[:], scalar1=0.0, scalar2=-scale, op0=ALU.max, op1=ALU.mult
            )
            rsc = small.tile([P, 2], F32, name="rsc", tag="rsc")
            nc.vector.tensor_scalar(
                out=rsc[:], in0=m[:], scalar1=0.0, scalar2=scale, op0=ALU.is_ge, op1=ALU.mult
            )
            st[("negm", j)] = negm
            st[("rsc", j)] = rsc

        def exp_row(s):
            h, rl = divmod(s, 4)
            if rl == 0:
                st[("ssum", h)] = small.tile([P, 4], F32, name="ssum", tag="ssum")
            ebf = work.tile([P, N], BF16, name="ebf", tag="ebf", bufs=4)
            nc.scalar.activation(
                out=ebf[:], in_=st[("z", s)][:], func=ACT.Exp,
                bias=st[("negm", s // 2)][:, s % 2 : s % 2 + 1], scale=st[("rsc", s // 2)][:, s % 2 : s % 2 + 1],
                accum_out=st[("ssum", h)][:, rl : rl + 1],
            )
            st[("ebf", s)] = ebf

        def e_transposes(s):
            tp = ps_t.tile([P, NRB // 2, P], F32, name="tp", tag="tp")
            ew = st[("ebf", s)][:].bitcast(F32)
            for k in range(NRB // 2):
                nc.tensor.transpose(tp[:, k, :], ew[:, k * P : (k + 1) * P], ident_f[:])
            st[("tp", s)] = tp

        def e_regroup(s):
            h, rl = divmod(s, 4)
            if rl == 0:
                st[("grp", h)] = mxp.tile([P, 8 * HALF], BF16, name="grp", tag="grp", align_bytes=64)
            gw = st[("grp", h)][:].bitcast(F32).rearrange("p (g i u) -> p g i u", g=2, u=2)
            nc.scalar.copy(
                out=gw[:, :, rl * P : (rl + 1) * P, :],
                in_=st[("tp", s)][:].rearrange("p (g u) i -> p g i u", g=2),
            )

        def e_quant(h, g):
            if g == 0:
                st[("ecod", h)] = mxp.tile([P, 2 * HALF], U32, name="ecod", tag="ecod", align_bytes=64)
                st[("esc", h)] = mxp.tile([P, 2 * HALF], U8, name="esc", tag="esc", align_bytes=64)
            cols = slice(g * HALF, (g + 1) * HALF)
            nc.vector.quantize_mx(
                out=st[("ecod", h)][:, cols].bitcast(FP8X4), scales=st[("esc", h)][:, cols],
                in_=st[("grp", h)][:, g * 4 * HALF : (g + 1) * 4 * HALF],
            )

        def f_transposes(b, g, cp):
            xw = xs[b][:].rearrange("p cc n -> p (cc n)").bitcast(F32)
            ft = ps_t.tile([P, 2, 2 * P], F32, name="ft", tag="tp")
            for u in range(2):
                for c2 in range(2):
                    w0 = (2 * cp + c2) * (N // 2) + (2 * g + u) * P
                    nc.tensor.transpose(ft[:, u, c2 * P : (c2 + 1) * P], xw[:, w0 : w0 + P], ident_f[:])
            st[("ft", b, g, cp)] = ft

        def f_regroup(b, g, cp):
            if g == 0 and cp == 0:
                st[("fgrp", b)] = mxp.tile([P, 4 * N], BF16, name="fgrp", tag="fgrp", align_bytes=64)
            fgw = st[("fgrp", b)][:].bitcast(F32).rearrange("p (g c u) -> p g c u", g=2, u=2)
            nc.scalar.copy(
                out=fgw[:, g, cp * 2 * P : (cp + 1) * 2 * P, :],
                in_=st[("ft", b, g, cp)][:].rearrange("p u c -> p c u"),
            )

        def f_quant(b, g):
            if g == 0:
                st[("fcod", b)] = mxp.tile([P, 2 * C], U32, name="fcod", tag="fcod", align_bytes=64)
                st[("fsc", b)] = mxp.tile([P, 2 * C], U8, name="fsc", tag="fsc", align_bytes=64)
            cols = slice(g * C, (g + 1) * C)
            nc.vector.quantize_mx(
                out=st[("fcod", b)][:, cols].bitcast(FP8X4), scales=st[("fsc", b)][:, cols],
                in_=st[("fgrp", b)][:, g * 4 * C : (g + 1) * 4 * C],
            )

        def rs_recip(h):
            rsv = small.tile([P, 4], F32, name="rsv", tag="rsv")
            nc.vector.reciprocal(out=rsv[:], in_=st[("ssum", h)][:])
            st[("rsv", h)] = rsv

        def rs_broadcast(h):
            rsv = st[("rsv", h)]
            bc = ps_t.tile([P, HALF], F32, name="bc", tag="tp")
            for rl in range(4):
                nc.tensor.transpose(
                    bc[:, rl * P : (rl + 1) * P], rsv[:, rl : rl + 1].to_broadcast([P, P]), ident_f[:]
                )
            st[("bc", h)] = bc

        def rs_copy(h):
            rsb = mxp.tile([P, HALF], F32, name="rsb", tag="rsb")
            nc.scalar.copy(out=rsb[:], in_=st[("bc", h)][:])
            st[("rsb", h)] = rsb

        def mx_block(h, cc):
            b = h // 2
            if h == 2 * B - 2:
                acc = ps_s.tile([P, HALF], F32, name="acc6", tag="sps")
            else:
                acc = ps_o.tile([P, HALF], F32, name="acc", tag="acc")
            for g in range(2):
                nc.tensor.matmul_mx(
                    out=acc[:],
                    lhsT=st[("fcod", b)][:, g * C + cc * P : g * C + (cc + 1) * P].bitcast(FP8X4),
                    lhsT_scale=st[("fsc", b)][:, g * C + cc * P : g * C + (cc + 1) * P],
                    rhs=st[("ecod", h)][:, g * HALF : (g + 1) * HALF].bitcast(FP8X4),
                    rhs_scale=st[("esc", h)][:, g * HALF : (g + 1) * HALF],
                    start=(g == 0),
                    stop=(g == 1),
                )
            st[("acc", h, cc)] = acc

        def drain_acc(h, cc):
            if cc == 0:
                st[("osb", h)] = work.tile([P, NCC, HALF], F32, name="osb", tag="osb")
            nc.scalar.copy(out=st[("osb", h)][:, cc, :], in_=st[("acc", h, cc)][:])

        def scale_gpsimd(h, cc):
            dst = st[("osb", h)][:, cc, :]
            nc.gpsimd.tensor_tensor(out=dst, in0=dst, in1=st[("rsb", h)][:], op=ALU.mult)
            store(h, cc)

        def scale_vector(h, cc):
            if cc == 0:
                st[("osb", h)] = work.tile([P, NCC, HALF], F32, name="osb", tag="osb")
            nc.vector.tensor_tensor(
                out=st[("osb", h)][:, cc, :], in0=st[("acc", h, cc)][:], in1=st[("rsb", h)][:], op=ALU.mult
            )
            store(h, cc)

        def store(h, cc):
            b, hh = divmod(h, 2)
            st[("left", h)] = st.get(("left", h), NCC) - 1
            if st[("left", h)] == 0:
                nc.sync.dma_start(out=ov[b][:, :, hh * HALF : (hh + 1) * HALF], in_=st[("osb", h)][:])

        def last_quant(s):
            h, rl = divmod(s, 4)
            if rl == 0:
                st[("ecod", h)] = mxp.tile([P, 2 * HALF], U32, name="ecod", tag="ecod", align_bytes=64)
                st[("esc", h)] = mxp.tile([P, 2 * HALF], U8, name="esc", tag="esc", align_bytes=64)
            for g in range(2):
                c0 = g * HALF + rl * P
                nc.vector.quantize_mx(
                    out=st[("ecod", h)][:, c0 : c0 + P].bitcast(FP8X4), scales=st[("esc", h)][:, c0 : c0 + P],
                    in_=st[("grp", h)][:, 4 * c0 : 4 * (c0 + P)],
                )

        def last_recip(s):
            h, rl = divmod(s, 4)
            if rl == 0:
                st[("rsv", h)] = small.tile([P, 4], F32, name="rsv", tag="rsv")
            nc.vector.reciprocal(out=st[("rsv", h)][:, rl : rl + 1], in_=st[("ssum", h)][:, rl : rl + 1])

        def last_broadcast(s):
            h, rl = divmod(s, 4)
            bc = ps_t.tile([P, HALF], F32, name="lbc", tag="tp")
            nc.tensor.transpose(bc[:, :P], st[("rsv", h)][:, rl : rl + 1].to_broadcast([P, P]), ident_f[:])
            st[("bc", s)] = bc

        def last_rs_copy(s):
            rsb = small.tile([P, P], F32, name="lrsb", tag="lrsb")
            nc.scalar.copy(out=rsb[:], in_=st[("bc", s)][:, :P])
            st[("lrsb", s)] = rsb

        def last_mx(s):
            h, rl = divmod(s, 4)
            b = h // 2
            acc = ps_o.tile([P, NCC, P], F32, name="lacc", tag="acc")
            for cc in range(NCC):
                for g in range(2):
                    f0 = g * C + cc * P
                    c0 = g * HALF + rl * P
                    nc.tensor.matmul_mx(
                        out=acc[:, cc, :],
                        lhsT=st[("fcod", b)][:, f0 : f0 + P].bitcast(FP8X4),
                        lhsT_scale=st[("fsc", b)][:, f0 : f0 + P],
                        rhs=st[("ecod", h)][:, c0 : c0 + P].bitcast(FP8X4),
                        rhs_scale=st[("esc", h)][:, c0 : c0 + P],
                        start=(g == 0),
                        stop=(g == 1),
                    )
            st[("lacc", s)] = acc

        def last_scale(s):
            b, r = divmod(s, NRB)
            osr = work.tile([P, NCC, P], F32, name="osr", tag="osr")
            nc.vector.tensor_tensor(
                out=osr[:], in0=st[("lacc", s)][:],
                in1=st[("lrsb", s)][:].unsqueeze(1).to_broadcast([P, NCC, P]), op=ALU.mult,
            )
            nc.sync.dma_start(out=ov[b][:, :, r * P : (r + 1) * P], in_=osr[:])

        NS = B * NRB
        NH = 2 * B
        ctx.enter_context(tc.manual_schedule())

        def at(t, lag):
            return divmod(t - lag, 4) if 0 <= t - lag < NS - 4 else (-1, -1)

        def rows(t, lag):
            s = t - lag
            if s == NS - 2:
                return [s, s + 1]
            return [s] if 0 <= s < NS - 2 else []

        def last_rows(t, lag):
            return [s for s in rows(t, lag) if s >= NS - 4]

        def blocks(t, lag):
            h, cc = at(t, lag)
            if h < 0:
                return []
            if h < NH - 2:
                return [(h, cc)]
            return [(h, 2 * cc), (h, 2 * cc + 1)] if cc < 2 else []

        for t in range(-2, NS + 10):
            for s in last_rows(t, 6):
                last_scale(s)
            for s in rows(t, 2):
                exp_row(s)
            if 0 <= t - 1 < NS and (t - 1) % 2 == 0:
                b, k = divmod((t - 1) // 2, 4)
                f_regroup(b, k // 2, k % 2)
            if 0 <= t - 0 < NS:
                exit_direct(t - 0)
            if 0 <= t - 0 < NS:
                s_mirror(t - 0)
            if 0 <= t + 1 < NS:
                s_matmuls(t + 1, 0, 0)
            for s in rows(t, 3):
                e_transposes(s)
            if 0 <= t + 1 < NS:
                s_matmuls(t + 1, 0, 1)
            if 0 <= t - 0 < NS and (t - 0) % 2 == 0:
                b, k = divmod((t - 0) // 2, 4)
                f_transposes(b, k // 2, k % 2)
            if 0 <= t + 1 < NS:
                s_matmuls(t + 1, 1, 0)
            h, cc = at(t, 7)
            if cc == 0:
                rs_broadcast(h)
            for s in last_rows(t, 5):
                last_mx(s)
            for h, cc in blocks(t, 8):
                mx_block(h, cc)
            if 0 <= t + 1 < NS:
                s_matmuls(t + 1, 1, 1)
            for s in rows(t, 3):
                e_regroup(s)
            for s in last_rows(t, 4):
                last_broadcast(s)
            for h, cc in blocks(t, 9):
                if (h < 5 and cc != 2):
                    drain_acc(h, cc)
            for s in last_rows(t, 4):
                last_rs_copy(s)
            h, cc = at(t, 7)
            if cc == 0:
                rs_copy(h)
            if 0 <= t - 0 < NS:
                exit_mirror(t - 0)
            for h, cc in blocks(t, 9):
                if not (h < 5 and cc != 2):
                    scale_vector(h, cc)
            if 0 <= t - 0 < NS and (t - 0) % 2 == 1:
                pair_max((t - 0) // 2)
            if 0 <= t - 0 < NS:
                steep_mask(t - 0)
            if 0 <= t - 0 < NS and (t - 0) % 2 == 1:
                pair_scalars((t - 0) // 2)
            h, cc = at(t, 6)
            if cc == 0:
                rs_recip(h)
            for s in last_rows(t, 3):
                last_recip(s)
            for s in last_rows(t, 4):
                last_quant(s)
            if 0 <= t - 5 < NS and (t - 5) % 8 == 0:
                f_quant((t - 5) // 8, 0)
            if 0 <= t - 7 < NS and (t - 7) % 8 == 0:
                f_quant((t - 7) // 8, 1)
            h, cc = at(t, 7)
            if cc == 0:
                e_quant(h, 0)
            h, cc = at(t, 7)
            if cc == 0:
                e_quant(h, 1)
            for h, cc in blocks(t, 9):
                if (h < 5 and cc != 2):
                    scale_gpsimd(h, cc)
